import numpy as np
import ml_dtypes


def mxq(x, axis, fmt="e4m3"):
    dtype, down = {"e4m3": (ml_dtypes.float8_e4m3fn, 7), "e5m2": (ml_dtypes.float8_e5m2, 14)}[fmt]
    v = np.moveaxis(np.asarray(x, np.float32).astype(ml_dtypes.bfloat16).astype(np.float64), axis, -1)
    blocks = v.reshape(v.shape[:-1] + (-1, 32))
    amax = np.abs(blocks).max(-1, keepdims=True)
    byte = np.maximum(np.where(amax > 0, np.frexp(amax)[1] - 1 + 127, 0) - down, 1)
    scale = np.exp2(byte - 127.0)
    codes = (blocks / scale).astype(np.float32).astype(dtype).astype(np.float64)
    return np.moveaxis((codes * scale).reshape(v.shape), -1, axis)


WIDE = False


def mx_kscale(k):
    if not WIDE:
        return np.ones(k)
    levels = np.array([10, -10, 5, -5, 0])
    a = np.random.permutation(np.resize(levels, k // 512 * 4)).reshape(k // 512, 4)
    idx = np.arange(k)
    return np.exp2(a[idx // 512, idx % 128 // 32])


BF16 = ml_dtypes.bfloat16


def bf(x):
    return np.asarray(x, np.float32).astype(BF16)


def f64(x):
    return np.asarray(x).astype(np.float64)


E2M1 = np.array([0.0, 0.5, 1.0, 1.5, 2.0, 3.0, 4.0, 6.0, -0.0, -0.5, -1.0, -1.5, -2.0, -3.0, -4.0, -6.0])


def pack_weight(w, fmt):
    k, n = w.shape
    w = f64(bf(w)).reshape(k // 32, 32, n)
    amax = np.abs(w).max(1)
    if fmt == "e4m3":
        byte = np.frexp(amax)[1] - 1 + 127 - 7
    else:
        mant, ex = np.frexp(amax / 6.0)
        byte = np.where(mant > 0.5, ex, ex - 1) + 127
    byte = np.clip(np.where(amax > 0, byte, 1), 1, 254)
    scaled = (w * np.exp2(127.0 - byte)[:, None, :]).reshape(k, n).astype(np.float32)
    by_word = np.ascontiguousarray(scaled.reshape(k // 512, 128, 4, n).transpose(0, 1, 3, 2))
    if fmt == "e4m3":
        words = by_word.astype(ml_dtypes.float8_e4m3fn).view(np.uint8)
    else:
        c = by_word.astype(ml_dtypes.float4_e2m1fn).view(np.uint8) & 0xF
        words = c[..., 0::2] | (c[..., 1::2] << 4)
    return np.ascontiguousarray(words), np.ascontiguousarray(byte.astype(np.uint8).reshape(k // 512, 16, n))


def unpack_weight(words, scales, fmt):
    g, p, n, _ = words.shape
    if fmt == "e4m3":
        vals = np.ascontiguousarray(words).view(ml_dtypes.float8_e4m3fn).astype(np.float64)
    else:
        nib = np.empty((g, p, n, 4), np.uint8)
        nib[..., 0::2] = words & 0xF
        nib[..., 1::2] = words >> 4
        vals = E2M1[nib]
    vals = vals * np.repeat(np.exp2(scales.astype(np.float64) - 127.0), 8, axis=1)[..., None]
    return vals.transpose(0, 1, 3, 2).reshape(g * 512, n)


B, M, N, P = 4, 2048, 1024, 128
EPS = 1e-05
FMT = "e4m3"


def normalize(v, axes, gamma, beta):
    mean = v.mean(axis=axes, keepdims=True)
    std = np.sqrt(v.var(axis=axes, keepdims=True, ddof=1))
    return gamma * ((v - mean) / (std + EPS)) + beta


def setup_inputs():
    s = mx_kscale(N)
    x = bf(np.random.standard_normal((B, M, N)) * s)
    xj_words, xj_scales = pack_weight(np.random.standard_normal((N, P)) * 0.5 / np.sqrt(N) / s[:, None], FMT)
    xi_words, xi_scales = pack_weight(np.random.standard_normal((M, P)) * 2.0 / np.sqrt(M), FMT)
    return {"x": x,
            "original_xj_y_words": xj_words,
            "original_xj_y_scales": xj_scales,
            "original_xi_y_words": xi_words,
            "original_xi_y_scales": xi_scales,
            "gamma_o_sum": bf(1.0 + 0.1 * np.random.standard_normal(P)),
            "gamma_o": bf(1.0 + 0.1 * np.random.standard_normal((P, P))),
            "beta_o_sum": bf(0.1 * np.random.standard_normal(P)),
            "beta_o": bf(0.1 * np.random.standard_normal((P, P)))}


def reference(x, original_xj_y_words, original_xj_y_scales, original_xi_y_words, original_xi_y_scales, gamma_o_sum, gamma_o, beta_o_sum, beta_o):
    oyy = mxq(f64(x), 2, "e4m3") @ unpack_weight(original_xj_y_words, original_xj_y_scales, FMT)
    o_sum = normalize(oyy.sum(axis=-2), (-1,), f64(gamma_o_sum), f64(beta_o_sum)) + 1.0
    oyy = mxq(np.swapaxes(oyy, -1, -2), 2, "e4m3") @ unpack_weight(original_xi_y_words, original_xi_y_scales, FMT)
    oyy = np.swapaxes(oyy, -1, -2)
    oyy = normalize(oyy, (-2, -1), f64(gamma_o), f64(beta_o))
    return oyy, o_sum

@@ -1,0 +1,295 @@
+from contextlib import ExitStack
+
+import concourse.mybir as mybir
+from concourse.masks import make_identity
+
+F32 = mybir.dt.float32
+BF16 = mybir.dt.bfloat16
+I32 = mybir.dt.int32
+U32 = mybir.dt.uint32
+U8 = mybir.dt.uint8
+FP8X4 = mybir.dt.float8_e4m3fn_x4
+ALU = mybir.AluOpType
+ACT = mybir.ActivationFunctionType
+AXIS = mybir.AxisListType
+
+P = 128
+PACK = 4
+K_PASS = P * PACK
+BATCH = 4
+ROWS = 2048
+K = 1024
+K_PASSES = K // K_PASS
+ROW_PASSES = ROWS // K_PASS
+BLOCKS = BATCH * ROW_PASSES
+PAIRS = 2
+WORDS_PASS = K_PASS // 2
+QUADRANTS = 4
+EPS = 1e-05
+HEAD_BLOCKS = 2
+
+FLOPS = 2 * BATCH * ROWS * K * P + 2 * BATCH * ROWS * P * P
+
+
+def tile_selfprojection_pa_t_kernel(
+    tc,
+    x,
+    original_xj_y_words,
+    original_xj_y_scales,
+    original_xi_y_words,
+    original_xi_y_scales,
+    gamma_o_sum,
+    gamma_o,
+    beta_o_sum,
+    beta_o,
+    out_0,
+    out_1,
+):
+    nc = tc.nc
+    with ExitStack() as ctx:
+        ctx.enter_context(tc.manual_schedule())
+        keep = ctx.enter_context(tc.tile_pool(name="keep", bufs=1))
+        x_pool = ctx.enter_context(tc.tile_pool(name="x_pool", bufs=BLOCKS))
+        stage = ctx.enter_context(tc.tile_pool(name="stage", bufs=4))
+        ring = ctx.enter_context(tc.tile_pool(name="ring", bufs=3))
+        flip_psum = ctx.enter_context(tc.psum_pool(name="flip_psum", bufs=4))
+        y_pool = ctx.enter_context(tc.psum_pool(name="y_pool", bufs=2))
+        z_pool = ctx.enter_context(tc.psum_pool(name="z_pool", bufs=1))
+        sums_pool = ctx.enter_context(tc.psum_pool(name="sums_pool", bufs=1))
+
+        xj_scales = keep.tile([P, K_PASSES, P], U8, align_bytes=64)
+        xi_scales = keep.tile([P, ROW_PASSES, P], U8, align_bytes=64)
+        nc.vector.memset(xj_scales[:].bitcast(I32), 0)
+        nc.vector.memset(xi_scales[:].bitcast(I32), 0)
+        ones = keep.tile([P, P], F32)
+        nc.vector.memset(ones[:], 1.0)
+        warm = keep.tile([P, 1], F32)
+        nc.vector.memset(warm[:], 1.0)
+        nc.scalar.activation(out=warm[:], in_=warm[:], func=ACT.Sqrt)
+        identity = keep.tile([P, P], F32)
+        make_identity(nc, identity[:])
+
+        x_blocks_hbm = x.rearrange("b (g p t) k -> (b g) p t k", p=P, t=PACK)
+        x_rows = []
+        for block in range(BLOCKS):
+            x_rows.append(x_pool.tile([P, PACK, K], BF16, name="x_rows"))
+
+        def load_block(block):
+            if block < HEAD_BLOCKS:
+                for t in range(PACK):
+                    nc.sync.dma_start(out=x_rows[block][:, t, :], in_=x_blocks_hbm[block, :, t, :])
+            else:
+                nc.sync.dma_start(out=x_rows[block][:], in_=x_blocks_hbm[block])
+
+        def load_weight(words_hbm, scales_hbm, codes, scales):
+            nc.sync.dma_start(
+                out=codes[:].bitcast(I32),
+                in_=words_hbm.rearrange("g p n t -> p g (n t)").bitcast(I32),
+            )
+            rows = scales_hbm.rearrange("g q n -> q g n")
+            for quadrant in range(QUADRANTS):
+                nc.sync.dma_start(
+                    out=scales[32 * quadrant : 32 * quadrant + 4].bitcast(I32),
+                    in_=rows[4 * quadrant : 4 * quadrant + 4].bitcast(I32),
+                )
+
+        xj_codes = keep.tile([P, K_PASSES, P], U32, align_bytes=64)
+        xi_codes = keep.tile([P, ROW_PASSES, P], U32, align_bytes=64)
+        gain = keep.tile([P, P], BF16)
+        bias = keep.tile([P, P], BF16)
+        gain_sum = keep.tile([1, P], BF16)
+        bias_sum = keep.tile([1, P], BF16)
+
+        load_block(0)
+        load_weight(original_xj_y_words, original_xj_y_scales, xj_codes, xj_scales)
+        load_block(1)
+        load_weight(original_xi_y_words, original_xi_y_scales, xi_codes, xi_scales)
+        load_block(2)
+        nc.sync.dma_start(out=gain[:], in_=gamma_o)
+        nc.sync.dma_start(out=bias[:], in_=beta_o)
+        nc.sync.dma_start(out=gain_sum[:], in_=gamma_o_sum.rearrange("(o j) -> o j", o=1))
+        nc.sync.dma_start(out=bias_sum[:], in_=beta_o_sum.rearrange("(o j) -> o j", o=1))
+        for block in range(3, BLOCKS):
+            load_block(block)
+
+        x_codes = {}
+        x_scales = {}
+        y_codes = {}
+        y_scales = {}
+        column_sums = {}
+        z_psum = {}
+
+        def transpose_block(block):
+            x_codes[block] = ring.tile([P, PACK, K_PASSES, P], U32, name="x_codes", align_bytes=64)
+            x_scales[block] = ring.tile([P, PACK, K_PASSES, P], U8, name="x_scales", align_bytes=64)
+            for t in range(PACK):
+                words = x_rows[block][:, t, :].bitcast(F32)
+                flipped = flip_psum.tile([P, K_PASSES, PAIRS, P], F32, name="flipped")
+                for g in range(K_PASSES):
+                    for u in range(PAIRS):
+                        nc.tensor.transpose(
+                            flipped[:, g, u, :],
+                            words[:, WORDS_PASS * g + u : WORDS_PASS * (g + 1) : PAIRS],
+                            identity[:],
+                        )
+                grouped = stage.tile([P, K_PASSES, P, PACK], BF16, name="grouped", align_bytes=64)
+                nc.scalar.copy(out=grouped[:].bitcast(F32), in_=flipped[:].rearrange("p g u r -> p g r u"))
+                nc.vector.quantize_mx(
+                    out=x_codes[block][:, t].rearrange("p g r -> p (g r)").bitcast(FP8X4),
+                    scales=x_scales[block][:, t].rearrange("p g r -> p (g r)"),
+                    in_=grouped[:].rearrange("p g r v -> p (g r v)"),
+                )
+
+        def project_block(block):
+            batch, row_pass = divmod(block, ROW_PASSES)
+            y_psum = y_pool.tile([P, PACK, P], F32, name="y_psum")
+            for t in range(PACK):
+                for g in range(K_PASSES):
+                    nc.tensor.matmul_mx(
+                        out=y_psum[:, t, :],
+                        lhsT=x_codes[block][:, t, g, :].bitcast(FP8X4),
+                        lhsT_scale=x_scales[block][:, t, g, :],
+                        rhs=xj_codes[:, g, :].bitcast(FP8X4),
+                        rhs_scale=xj_scales[:, g, :],
+                        start=(g == 0),
+                        stop=(g == K_PASSES - 1),
+                    )
+            by_column = y_psum[:].rearrange("p t j -> p j t")
+            y_grouped = stage.tile([P, P, PACK], BF16, name="y_grouped", align_bytes=64)
+            nc.vector.tensor_copy(out=y_grouped[:], in_=by_column)
+            if row_pass == 0:
+                column_sums[batch] = ring.tile([P, P], F32, name="column_sums")
+                nc.vector.tensor_reduce(out=column_sums[batch][:], in_=by_column, axis=AXIS.X, op=ALU.add)
+            else:
+                block_sums = ring.tile([P, P], F32, name="block_sums")
+                nc.vector.tensor_reduce(out=block_sums[:], in_=by_column, axis=AXIS.X, op=ALU.add)
+                nc.gpsimd.tensor_tensor(
+                    out=column_sums[batch][:], in0=column_sums[batch][:], in1=block_sums[:], op=ALU.add
+                )
+            y_codes[block] = ring.tile([P, P], U32, name="y_codes", align_bytes=64)
+            y_scales[block] = ring.tile([P, P], U8, name="y_scales", align_bytes=64)
+            nc.vector.quantize_mx(
+                out=y_codes[block][:].bitcast(FP8X4),
+                scales=y_scales[block][:],
+                in_=y_grouped[:].rearrange("p j t -> p (j t)"),
+            )
+
+        def contract_block(block):
+            batch, row_pass = divmod(block, ROW_PASSES)
+            if row_pass == 0:
+                z_psum[batch] = z_pool.tile([P, P], F32, name="z_psum")
+            nc.tensor.matmul_mx(
+                out=z_psum[batch][:],
+                lhsT=xi_codes[:, row_pass, :].bitcast(FP8X4),
+                lhsT_scale=xi_scales[:, row_pass, :],
+                rhs=y_codes[block][:].bitcast(FP8X4),
+                rhs_scale=y_scales[block][:],
+                start=(row_pass == 0),
+                stop=(row_pass == ROW_PASSES - 1),
+            )
+
+        z_count = P * P
+        sums_psum = {}
+        z_sbuf = {}
+        row_sum = {}
+        neg_mean = {}
+        row_squares = {}
+        z_gained = {}
+        c_stats = {}
+        o_sum_rows = keep.tile([1, BATCH * P], F32)
+
+        def stage_row_sums(batch):
+            sums_psum[batch] = sums_pool.tile([P, P + 2], F32, name="sums_psum")
+            nc.tensor.matmul(
+                out=sums_psum[batch][:, 0:P], lhsT=ones[:], rhs=column_sums[batch][:], start=True, stop=True
+            )
+            z_sbuf[batch] = ring.tile([P, P], F32, name="z_sbuf")
+            row_sum[batch] = ring.tile([P, 1], F32, name="row_sum")
+            nc.scalar.activation(
+                out=z_sbuf[batch][:], in_=z_psum[batch][:], func=ACT.Identity, accum_out=row_sum[batch][:]
+            )
+
+        def stage_total(batch):
+            nc.tensor.matmul(
+                out=sums_psum[batch][:, P : P + 1], lhsT=ones[:], rhs=row_sum[batch][:], start=True, stop=True
+            )
+            six = ring.tile([1, 6], F32, name="six")
+            nc.vector.bn_stats(out=six[:], in_=sums_psum[batch][0:1, 0:P])
+            c_stats[batch] = ring.tile([1, 2], F32, name="c_stats")
+            nc.vector.bn_aggr(out=c_stats[batch][:], in_=six[:])
+
+        def stage_centre(batch):
+            neg_mean[batch] = ring.tile([P, 1], F32, name="neg_mean")
+            nc.scalar.activation(
+                out=neg_mean[batch][:], in_=sums_psum[batch][:, P : P + 1], func=ACT.Copy, scale=-1.0 / z_count
+            )
+            squares = ring.tile([P, P], F32, name="squares")
+            row_squares[batch] = ring.tile([P, 1], F32, name="row_squares")
+            nc.scalar.activation(
+                out=squares[:],
+                in_=z_sbuf[batch][:],
+                func=ACT.Square,
+                bias=neg_mean[batch][:],
+                accum_out=row_squares[batch][:],
+            )
+            c_spread = ring.tile([1, 1], F32, name="c_spread")
+            nc.scalar.activation(out=c_spread[:], in_=c_stats[batch][:, 1:2], func=ACT.Sqrt, scale=P / (P - 1.0))
+            z_gained[batch] = ring.tile([P, P], F32, name="z_gained")
+            nc.vector.scalar_tensor_tensor(
+                out=z_gained[batch][:],
+                in0=z_sbuf[batch][:],
+                scalar=neg_mean[batch][:],
+                in1=gain[:],
+                op0=ALU.add,
+                op1=ALU.mult,
+            )
+            c_gained = ring.tile([1, P], F32, name="c_gained")
+            nc.vector.scalar_tensor_tensor(
+                out=c_gained[:],
+                in0=sums_psum[batch][0:1, 0:P],
+                scalar=c_stats[batch][:, 0:1],
+                in1=gain_sum[:],
+                op0=ALU.subtract,
+                op1=ALU.mult,
+            )
+            nc.vector.tensor_scalar_add(out=c_spread[:], in0=c_spread[:], scalar1=EPS)
+            nc.vector.reciprocal(out=c_spread[:], in_=c_spread[:])
+            o_sum_row = o_sum_rows[:, P * batch : P * (batch + 1)]
+            nc.vector.scalar_tensor_tensor(
+                out=o_sum_row, in0=c_gained[:], scalar=c_spread[:], in1=bias_sum[:], op0=ALU.mult, op1=ALU.add
+            )
+            nc.vector.tensor_scalar_add(out=o_sum_row, in0=o_sum_row, scalar1=1.0)
+            if batch == BATCH - 1:
+                nc.sync.dma_start(out=out_1.rearrange("(o b) j -> o (b j)", o=1), in_=o_sum_rows[:])
+
+        def stage_total_squares(batch):
+            nc.tensor.matmul(
+                out=sums_psum[batch][:, P + 1 : P + 2], lhsT=ones[:], rhs=row_squares[batch][:], start=True, stop=True
+            )
+
+        def stage_finish(batch):
+            z_spread = ring.tile([P, 1], F32, name="z_spread")
+            nc.scalar.activation(
+                out=z_spread[:], in_=sums_psum[batch][:, P + 1 : P + 2], func=ACT.Sqrt, scale=1.0 / (z_count - 1)
+            )
+            nc.vector.tensor_scalar_add(out=z_spread[:], in0=z_spread[:], scalar1=EPS)
+            nc.vector.reciprocal(out=z_spread[:], in_=z_spread[:])
+            result = ring.tile([P, P], F32, name="result")
+            nc.vector.scalar_tensor_tensor(
+                out=result[:], in0=z_gained[batch][:], scalar=z_spread[:], in1=bias[:], op0=ALU.mult, op1=ALU.add
+            )
+            nc.sync.dma_start(out=out_0[batch], in_=result[:])
+
+        stages = (stage_row_sums, stage_total, stage_centre, stage_total_squares, stage_finish)
+
+        for step in range(BLOCKS + 2 + len(stages) - 1):
+            if step < BLOCKS:
+                transpose_block(step)
+            if 0 <= step - 1 < BLOCKS:
+                project_block(step - 1)
+            if 0 <= step - 2 < BLOCKS:
+                contract_block(step - 2)
+            for lag in reversed(range(len(stages))):
+                block = step - 2 - lag
+                if 0 <= block < BLOCKS and block % ROW_PASSES == ROW_PASSES - 1:
+                    stages[lag](block // ROW_PASSES)

@@ -26,6 +26,10 @@ PAIRS = 2
 WORDS_PASS = K_PASS // 2
 QUADRANTS = 4
 EPS = 1e-05
+CHUNKS = K_PASSES * PAIRS
+WORDS_CHUNK = P
+HALF = P // 2
+FIRST_PROJECT = 2
 HEAD_BLOCKS = 2
 
 FLOPS = 2 * BATCH * ROWS * K * P + 2 * BATCH * ROWS * P * P
@@ -57,7 +61,7 @@ def tile_selfprojection_pa_t_kernel(
         z_pool = ctx.enter_context(tc.psum_pool(name="z_pool", bufs=1))
         sums_pool = ctx.enter_context(tc.psum_pool(name="sums_pool", bufs=1))
 
-        xj_scales = keep.tile([P, K_PASSES, P], U8, align_bytes=64)
+        xj_scales = keep.tile([P, CHUNKS, P], U8, align_bytes=64)
         xi_scales = keep.tile([P, ROW_PASSES, P], U8, align_bytes=64)
         nc.vector.memset(xj_scales[:].bitcast(I32), 0)
         nc.vector.memset(xi_scales[:].bitcast(I32), 0)
@@ -93,16 +97,39 @@ def tile_selfprojection_pa_t_kernel(
                     in_=rows[4 * quadrant : 4 * quadrant + 4].bitcast(I32),
                 )
 
-        xj_codes = keep.tile([P, K_PASSES, P], U32, align_bytes=64)
+        xj_raw = keep.tile([P, K_PASSES, P * PACK], U8, align_bytes=64)
+        xj_halves = keep.tile([P, PAIRS, K_PASSES, 2, P * PACK], U8, align_bytes=64)
+        xj_codes = keep.tile([P, CHUNKS, P * PACK], U8, align_bytes=64)
+        nc.vector.memset(xj_halves[:].bitcast(I32), 0)
         xi_codes = keep.tile([P, ROW_PASSES, P], U32, align_bytes=64)
         gain = keep.tile([P, P], BF16)
         bias = keep.tile([P, P], BF16)
         gain_sum = keep.tile([1, P], BF16)
         bias_sum = keep.tile([1, P], BF16)
 
+        nc.sync.dma_start(
+            out=xj_raw[:].bitcast(I32), in_=original_xj_y_words.rearrange("g p n t -> p g (n t)").bitcast(I32)
+        )
         load_block(0)
-        load_weight(original_xj_y_words, original_xj_y_scales, xj_codes, xj_scales)
+        rows = original_xj_y_scales.rearrange("g (h r) n -> r (g h) n", h=PAIRS)
+        for a in range(2):
+            for d in range(2):
+                nc.sync.dma_start(
+                    out=xj_scales[2 * a + d : P : 32].bitcast(I32), in_=rows[a:8:2].bitcast(I32)
+                )
+        for u in range(PAIRS):
+            for g in range(K_PASSES):
+                nc.vector.tensor_copy(
+                    out=xj_halves[:, u, g].rearrange("p h (n t) -> p n h t", t=PACK)[:, :, :, 2 * u : 2 * u + 2],
+                    in_=xj_raw[:, g, :].rearrange("p (n h e) -> p n h e", h=2, e=2),
+                )
         load_block(1)
+        for u in range(PAIRS):
+            for h in range(2):
+                nc.sync.dma_start(
+                    out=xj_codes[h:P:2, u:CHUNKS:2, :].bitcast(I32),
+                    in_=xj_halves[HALF * u : HALF * (u + 1), u, :, h, :].bitcast(I32),
+                )
         load_weight(original_xi_y_words, original_xi_y_scales, xi_codes, xi_scales)
         load_block(2)
         nc.sync.dma_start(out=gain[:], in_=gamma_o)
@@ -129,7 +156,7 @@ def tile_selfprojection_pa_t_kernel(
                     for u in range(PAIRS):
                         nc.tensor.transpose(
                             flipped[:, g, u, :],
-                            words[:, WORDS_PASS * g + u : WORDS_PASS * (g + 1) : PAIRS],
+                            words[:, WORDS_PASS * g + WORDS_CHUNK * u : WORDS_PASS * g + WORDS_CHUNK * (u + 1)],
                             identity[:],
                         )
                 grouped = stage.tile([P, K_PASSES, P, PACK], BF16, name="grouped", align_bytes=64)
@@ -144,15 +171,16 @@ def tile_selfprojection_pa_t_kernel(
             batch, row_pass = divmod(block, ROW_PASSES)
             y_psum = y_pool.tile([P, PACK, P], F32, name="y_psum")
             for t in range(PACK):
-                for g in range(K_PASSES):
+                for chunk in range(CHUNKS):
+                    g = chunk // PAIRS
                     nc.tensor.matmul_mx(
                         out=y_psum[:, t, :],
                         lhsT=x_codes[block][:, t, g, :].bitcast(FP8X4),
                         lhsT_scale=x_scales[block][:, t, g, :],
-                        rhs=xj_codes[:, g, :].bitcast(FP8X4),
-                        rhs_scale=xj_scales[:, g, :],
-                        start=(g == 0),
-                        stop=(g == K_PASSES - 1),
+                        rhs=xj_codes[:, chunk, :].bitcast(FP8X4),
+                        rhs_scale=xj_scales[:, chunk, :],
+                        start=(chunk == 0),
+                        stop=(chunk == CHUNKS - 1),
                     )
             by_column = y_psum[:].rearrange("p t j -> p j t")
             y_grouped = stage.tile([P, P, PACK], BF16, name="y_grouped", align_bytes=64)
@@ -285,10 +313,12 @@ def tile_selfprojection_pa_t_kernel(
         for step in range(BLOCKS + 2 + len(stages) - 1):
             if step < BLOCKS:
                 transpose_block(step)
-            if 0 <= step - 1 < BLOCKS:
-                project_block(step - 1)
-            if 0 <= step - 2 < BLOCKS:
-                contract_block(step - 2)
+            for block in range(BLOCKS):
+                if step == max(block + 1, FIRST_PROJECT):
+                    project_block(block)
+            for block in range(BLOCKS):
+                if step == max(block + 2, FIRST_PROJECT + 1):
+                    contract_block(block)
             for lag in reversed(range(len(stages))):
                 block = step - 2 - lag
                 if 0 <= block < BLOCKS and block % ROW_PASSES == ROW_PASSES - 1:

@@ -1,3 +1,4 @@
+import functools
 from contextlib import ExitStack
 
 import concourse.mybir as mybir
@@ -141,12 +142,14 @@ def tile_selfprojection_pa_t_kernel(
 
         x_codes = {}
         x_scales = {}
+        y_by_column = {}
+        y_grouped = {}
         y_codes = {}
         y_scales = {}
         column_sums = {}
         z_psum = {}
 
-        def transpose_block(block):
+        def transpose_block(block, chores):
             x_codes[block] = ring.tile([P, PACK, K_PASSES, P], U32, name="x_codes", align_bytes=64)
             x_scales[block] = ring.tile([P, PACK, K_PASSES, P], U8, name="x_scales", align_bytes=64)
             for t in range(PACK):
@@ -166,10 +169,13 @@ def tile_selfprojection_pa_t_kernel(
                     scales=x_scales[block][:, t].rearrange("p g r -> p (g r)"),
                     in_=grouped[:].rearrange("p g r v -> p (g r v)"),
                 )
+                if t < 3:
+                    for chore in chores[t * len(chores) // 3 : (t + 1) * len(chores) // 3]:
+                        chore()
 
         def project_block(block):
-            batch, row_pass = divmod(block, ROW_PASSES)
             y_psum = y_pool.tile([P, PACK, P], F32, name="y_psum")
+            y_by_column[block] = y_psum[:].rearrange("p t j -> p j t")
             for t in range(PACK):
                 for chunk in range(CHUNKS):
                     g = chunk // PAIRS
@@ -182,9 +188,17 @@ def tile_selfprojection_pa_t_kernel(
                         start=(chunk == 0),
                         stop=(chunk == CHUNKS - 1),
                     )
-            by_column = y_psum[:].rearrange("p t j -> p j t")
-            y_grouped = stage.tile([P, P, PACK], BF16, name="y_grouped", align_bytes=64)
-            nc.vector.tensor_copy(out=y_grouped[:], in_=by_column)
+
+        def round_y(block):
+            y_grouped[block] = stage.tile([P, P, PACK], BF16, name="y_rounded", align_bytes=64)
+            if block % 2:
+                nc.scalar.copy(out=y_grouped[block][:], in_=y_by_column[block])
+            else:
+                nc.vector.tensor_copy(out=y_grouped[block][:], in_=y_by_column[block])
+
+        def sum_y(block):
+            batch, row_pass = divmod(block, ROW_PASSES)
+            by_column = y_by_column[block]
             if row_pass == 0:
                 column_sums[batch] = ring.tile([P, P], F32, name="column_sums")
                 nc.vector.tensor_reduce(out=column_sums[batch][:], in_=by_column, axis=AXIS.X, op=ALU.add)
@@ -194,12 +208,14 @@ def tile_selfprojection_pa_t_kernel(
                 nc.gpsimd.tensor_tensor(
                     out=column_sums[batch][:], in0=column_sums[batch][:], in1=block_sums[:], op=ALU.add
                 )
+
+        def quantize_y(block):
             y_codes[block] = ring.tile([P, P], U32, name="y_codes", align_bytes=64)
             y_scales[block] = ring.tile([P, P], U8, name="y_scales", align_bytes=64)
             nc.vector.quantize_mx(
                 out=y_codes[block][:].bitcast(FP8X4),
                 scales=y_scales[block][:],
-                in_=y_grouped[:].rearrange("p j t -> p (j t)"),
+                in_=y_grouped[block][:].rearrange("p j t -> p (j t)"),
             )
 
         def contract_block(block):
@@ -310,16 +326,30 @@ def tile_selfprojection_pa_t_kernel(
 
         stages = (stage_row_sums, stage_total, stage_centre, stage_total_squares, stage_finish)
 
-        for step in range(BLOCKS + 2 + len(stages) - 1):
+        def y_step(block):
+            return max(block + 2, FIRST_PROJECT + 1)
+
+        def contract_step(block):
+            return y_step(block) + (1 if block < BLOCKS - 1 else 0)
+
+        for step in range(contract_step(BLOCKS - 1) + len(stages)):
+            chores = []
+            for block in range(BLOCKS):
+                if step == y_step(block):
+                    for chore in (round_y, quantize_y, sum_y) if block == BLOCKS - 1 else (round_y, sum_y, quantize_y):
+                        chores.append(functools.partial(chore, block))
             if step < BLOCKS:
-                transpose_block(step)
+                transpose_block(step, chores)
+            else:
+                for chore in chores:
+                    chore()
             for block in range(BLOCKS):
                 if step == max(block + 1, FIRST_PROJECT):
                     project_block(block)
             for block in range(BLOCKS):
-                if step == max(block + 2, FIRST_PROJECT + 1):
+                if step == contract_step(block):
                     contract_block(block)
             for lag in reversed(range(len(stages))):
-                block = step - 2 - lag
-                if 0 <= block < BLOCKS and block % ROW_PASSES == ROW_PASSES - 1:
-                    stages[lag](block // ROW_PASSES)
+                for batch in range(BATCH):
+                    if step == contract_step(ROW_PASSES * (batch + 1) - 1) + lag:
+                        stages[lag](batch)

@@ -30,8 +30,9 @@ EPS = 1e-05
 CHUNKS = K_PASSES * PAIRS
 WORDS_CHUNK = P
 HALF = P // 2
-FIRST_PROJECT = 2
-HEAD_BLOCKS = 2
+FIRST_PROJECT = 1
+EARLY = 3
+HEAD_BLOCKS = 1
 
 FLOPS = 2 * BATCH * ROWS * K * P + 2 * BATCH * ROWS * P * P
 
@@ -62,9 +63,11 @@ def tile_selfprojection_pa_t_kernel(
         z_pool = ctx.enter_context(tc.psum_pool(name="z_pool", bufs=1))
         sums_pool = ctx.enter_context(tc.psum_pool(name="sums_pool", bufs=1))
 
-        xj_scales = keep.tile([P, CHUNKS, P], U8, align_bytes=64)
+        xj_scales = keep.tile([P, K_PASSES, P], U8, align_bytes=64)
+        chunk_scales = keep.tile([P, CHUNKS, P], U8, align_bytes=64)
         xi_scales = keep.tile([P, ROW_PASSES, P], U8, align_bytes=64)
         nc.vector.memset(xj_scales[:].bitcast(I32), 0)
+        nc.vector.memset(chunk_scales[:].bitcast(I32), 0)
         nc.vector.memset(xi_scales[:].bitcast(I32), 0)
         ones = keep.tile([P, P], F32)
         nc.vector.memset(ones[:], 1.0)
@@ -86,11 +89,13 @@ def tile_selfprojection_pa_t_kernel(
             else:
                 nc.sync.dma_start(out=x_rows[block][:], in_=x_blocks_hbm[block])
 
-        def load_weight(words_hbm, scales_hbm, codes, scales):
+        def load_codes(words_hbm, codes):
             nc.sync.dma_start(
                 out=codes[:].bitcast(I32),
                 in_=words_hbm.rearrange("g p n t -> p g (n t)").bitcast(I32),
             )
+
+        def load_scales(scales_hbm, scales):
             rows = scales_hbm.rearrange("g q n -> q g n")
             for quadrant in range(QUADRANTS):
                 nc.sync.dma_start(
@@ -98,47 +103,52 @@ def tile_selfprojection_pa_t_kernel(
                     in_=rows[4 * quadrant : 4 * quadrant + 4].bitcast(I32),
                 )
 
-        xj_raw = keep.tile([P, K_PASSES, P * PACK], U8, align_bytes=64)
-        xj_halves = keep.tile([P, PAIRS, K_PASSES, 2, P * PACK], U8, align_bytes=64)
-        xj_codes = keep.tile([P, CHUNKS, P * PACK], U8, align_bytes=64)
-        nc.vector.memset(xj_halves[:].bitcast(I32), 0)
+        xj_codes = keep.tile([P, K_PASSES, P * PACK], U8, align_bytes=64)
+        halves = keep.tile([P, PAIRS, K_PASSES, 2, P * PACK], U8, align_bytes=64)
+        chunk_codes = keep.tile([P, CHUNKS, P * PACK], U8, align_bytes=64)
         xi_codes = keep.tile([P, ROW_PASSES, P], U32, align_bytes=64)
         gain = keep.tile([P, P], BF16)
         bias = keep.tile([P, P], BF16)
         gain_sum = keep.tile([1, P], BF16)
         bias_sum = keep.tile([1, P], BF16)
+        nc.vector.memset(halves[:].bitcast(I32), 0)
 
-        nc.sync.dma_start(
-            out=xj_raw[:].bitcast(I32), in_=original_xj_y_words.rearrange("g p n t -> p g (n t)").bitcast(I32)
-        )
+        def split_halves(u, g):
+            nc.vector.tensor_copy(
+                out=halves[:, u, g].rearrange("p h (n t) -> p n h t", t=PACK)[:, :, :, 2 * u : 2 * u + 2],
+                in_=xj_codes[:, g, :].rearrange("p (n h e) -> p n h e", h=2, e=2),
+            )
+
+        load_codes(original_xj_y_words, xj_codes)
+        load_scales(original_xj_y_scales, xj_scales)
         load_block(0)
+        load_block(1)
+        load_block(2)
         rows = original_xj_y_scales.rearrange("g (h r) n -> r (g h) n", h=PAIRS)
         for a in range(2):
             for d in range(2):
                 nc.sync.dma_start(
-                    out=xj_scales[2 * a + d : P : 32].bitcast(I32), in_=rows[a:8:2].bitcast(I32)
+                    out=chunk_scales[2 * a + d : P : 32].bitcast(I32), in_=rows[a:8:2].bitcast(I32)
                 )
-        for u in range(PAIRS):
-            for g in range(K_PASSES):
-                nc.vector.tensor_copy(
-                    out=xj_halves[:, u, g].rearrange("p h (n t) -> p n h t", t=PACK)[:, :, :, 2 * u : 2 * u + 2],
-                    in_=xj_raw[:, g, :].rearrange("p (n h e) -> p n h e", h=2, e=2),
-                )
-        load_block(1)
-        for u in range(PAIRS):
-            for h in range(2):
-                nc.sync.dma_start(
-                    out=xj_codes[h:P:2, u:CHUNKS:2, :].bitcast(I32),
-                    in_=xj_halves[HALF * u : HALF * (u + 1), u, :, h, :].bitcast(I32),
-                )
-        load_weight(original_xi_y_words, original_xi_y_scales, xi_codes, xi_scales)
-        load_block(2)
-        nc.sync.dma_start(out=gain[:], in_=gamma_o)
-        nc.sync.dma_start(out=bias[:], in_=beta_o)
-        nc.sync.dma_start(out=gain_sum[:], in_=gamma_o_sum.rearrange("(o j) -> o j", o=1))
-        nc.sync.dma_start(out=bias_sum[:], in_=beta_o_sum.rearrange("(o j) -> o j", o=1))
-        for block in range(3, BLOCKS):
-            load_block(block)
+        load_block(3)
+
+        def load_rest():
+            for u in range(PAIRS):
+                for h in range(2):
+                    nc.sync.dma_start(
+                        out=chunk_codes[h:P:2, u:CHUNKS:2, :].bitcast(I32),
+                        in_=halves[HALF * u : HALF * (u + 1), u, :, h, :].bitcast(I32),
+                    )
+            load_codes(original_xi_y_words, xi_codes)
+            load_scales(original_xi_y_scales, xi_scales)
+            load_block(4)
+            load_block(5)
+            nc.sync.dma_start(out=gain[:], in_=gamma_o)
+            nc.sync.dma_start(out=bias[:], in_=beta_o)
+            nc.sync.dma_start(out=gain_sum[:], in_=gamma_o_sum.rearrange("(o j) -> o j", o=1))
+            nc.sync.dma_start(out=bias_sum[:], in_=beta_o_sum.rearrange("(o j) -> o j", o=1))
+            for block in range(6, BLOCKS):
+                load_block(block)
 
         x_codes = {}
         x_scales = {}
@@ -157,11 +167,11 @@ def tile_selfprojection_pa_t_kernel(
                 flipped = flip_psum.tile([P, K_PASSES, PAIRS, P], F32, name="flipped")
                 for g in range(K_PASSES):
                     for u in range(PAIRS):
-                        nc.tensor.transpose(
-                            flipped[:, g, u, :],
-                            words[:, WORDS_PASS * g + WORDS_CHUNK * u : WORDS_PASS * g + WORDS_CHUNK * (u + 1)],
-                            identity[:],
-                        )
+                        if block < EARLY:
+                            part = words[:, WORDS_PASS * g + u : WORDS_PASS * (g + 1) : PAIRS]
+                        else:
+                            part = words[:, WORDS_PASS * g + WORDS_CHUNK * u : WORDS_PASS * g + WORDS_CHUNK * (u + 1)]
+                        nc.tensor.transpose(flipped[:, g, u, :], part, identity[:])
                 grouped = stage.tile([P, K_PASSES, P, PACK], BF16, name="grouped", align_bytes=64)
                 nc.scalar.copy(out=grouped[:].bitcast(F32), in_=flipped[:].rearrange("p g u r -> p g r u"))
                 nc.vector.quantize_mx(
@@ -177,16 +187,18 @@ def tile_selfprojection_pa_t_kernel(
             y_psum = y_pool.tile([P, PACK, P], F32, name="y_psum")
             y_by_column[block] = y_psum[:].rearrange("p t j -> p j t")
             for t in range(PACK):
-                for chunk in range(CHUNKS):
-                    g = chunk // PAIRS
+                codes, scales = (xj_codes, xj_scales) if block < EARLY else (chunk_codes, chunk_scales)
+                passes = K_PASSES if block < EARLY else CHUNKS
+                for i in range(passes):
+                    g = i * K_PASSES // passes
                     nc.tensor.matmul_mx(
                         out=y_psum[:, t, :],
                         lhsT=x_codes[block][:, t, g, :].bitcast(FP8X4),
                         lhsT_scale=x_scales[block][:, t, g, :],
-                        rhs=xj_codes[:, chunk, :].bitcast(FP8X4),
-                        rhs_scale=xj_scales[:, chunk, :],
-                        start=(chunk == 0),
-                        stop=(chunk == CHUNKS - 1),
+                        rhs=codes[:, i, :].bitcast(FP8X4),
+                        rhs_scale=scales[:, i, :],
+                        start=(i == 0),
+                        stop=(i == passes - 1),
                     )
 
         def round_y(block):
@@ -338,8 +350,14 @@ def tile_selfprojection_pa_t_kernel(
                 if step == y_step(block):
                     for chore in (round_y, quantize_y, sum_y) if block == BLOCKS - 1 else (round_y, sum_y, quantize_y):
                         chores.append(functools.partial(chore, block))
+            if step == 0:
+                for u in range(PAIRS):
+                    for g in range(K_PASSES):
+                        chores.append(functools.partial(split_halves, u, g))
             if step < BLOCKS:
                 transpose_block(step, chores)
+                if step == 0:
+                    load_rest()
             else:
                 for chore in chores:
                     chore()

@@ -32,7 +32,6 @@ WORDS_CHUNK = P
 HALF = P // 2
 FIRST_PROJECT = 1
 EARLY = 3
-HEAD_BLOCKS = 1
 
 FLOPS = 2 * BATCH * ROWS * K * P + 2 * BATCH * ROWS * P * P
 
@@ -71,23 +70,29 @@ def tile_selfprojection_pa_t_kernel(
         nc.vector.memset(xi_scales[:].bitcast(I32), 0)
         ones = keep.tile([P, P], F32)
         nc.vector.memset(ones[:], 1.0)
+        selector = keep.tile([P, 2 * P - 1], F32)
+        nc.vector.memset(selector[:], 0.0)
+        nc.vector.memset(selector[:, P - 1 : P], 1.0)
         warm = keep.tile([P, 1], F32)
         nc.vector.memset(warm[:], 1.0)
         nc.scalar.activation(out=warm[:], in_=warm[:], func=ACT.Sqrt)
         identity = keep.tile([P, P], F32)
         make_identity(nc, identity[:])
+        average = keep.tile([P, P], F32)
+        nc.vector.memset(average[:], 1.0 / P)
+        centre = keep.tile([P, P], F32)
+        nc.vector.tensor_tensor(out=centre[:], in0=identity[:], in1=average[:], op=ALU.subtract)
 
         x_blocks_hbm = x.rearrange("b (g p t) k -> (b g) p t k", p=P, t=PACK)
         x_rows = []
         for block in range(BLOCKS):
             x_rows.append(x_pool.tile([P, PACK, K], BF16, name="x_rows"))
 
+        def load_quarter(block, t):
+            nc.sync.dma_start(out=x_rows[block][:, t, :], in_=x_blocks_hbm[block, :, t, :])
+
         def load_block(block):
-            if block < HEAD_BLOCKS:
-                for t in range(PACK):
-                    nc.sync.dma_start(out=x_rows[block][:, t, :], in_=x_blocks_hbm[block, :, t, :])
-            else:
-                nc.sync.dma_start(out=x_rows[block][:], in_=x_blocks_hbm[block])
+            nc.sync.dma_start(out=x_rows[block][:], in_=x_blocks_hbm[block])
 
         def load_codes(words_hbm, codes):
             nc.sync.dma_start(
@@ -109,8 +114,9 @@ def tile_selfprojection_pa_t_kernel(
         xi_codes = keep.tile([P, ROW_PASSES, P], U32, align_bytes=64)
         gain = keep.tile([P, P], BF16)
         bias = keep.tile([P, P], BF16)
-        gain_sum = keep.tile([1, P], BF16)
-        bias_sum = keep.tile([1, P], BF16)
+        gain_sum = keep.tile([BATCH, P], BF16)
+        bias_sum = keep.tile([BATCH, P], BF16)
+        bias_sum_one = keep.tile([BATCH, P], F32)
         nc.vector.memset(halves[:].bitcast(I32), 0)
 
         def split_halves(u, g):
@@ -119,10 +125,13 @@ def tile_selfprojection_pa_t_kernel(
                 in_=xj_codes[:, g, :].rearrange("p (n h e) -> p n h e", h=2, e=2),
             )
 
+        load_quarter(0, 0)
         load_codes(original_xj_y_words, xj_codes)
         load_scales(original_xj_y_scales, xj_scales)
-        load_block(0)
-        load_block(1)
+        for t in range(1, PACK):
+            load_quarter(0, t)
+        for t in range(PACK):
+            load_quarter(1, t)
         load_block(2)
         rows = original_xj_y_scales.rearrange("g (h r) n -> r (g h) n", h=PAIRS)
         for a in range(2):
@@ -145,8 +154,8 @@ def tile_selfprojection_pa_t_kernel(
             load_block(5)
             nc.sync.dma_start(out=gain[:], in_=gamma_o)
             nc.sync.dma_start(out=bias[:], in_=beta_o)
-            nc.sync.dma_start(out=gain_sum[:], in_=gamma_o_sum.rearrange("(o j) -> o j", o=1))
-            nc.sync.dma_start(out=bias_sum[:], in_=beta_o_sum.rearrange("(o j) -> o j", o=1))
+            nc.sync.dma_start(out=gain_sum[:], in_=gamma_o_sum.partition_broadcast(BATCH))
+            nc.sync.dma_start(out=bias_sum[:], in_=beta_o_sum.partition_broadcast(BATCH))
             for block in range(6, BLOCKS):
                 load_block(block)
 
@@ -156,7 +165,7 @@ def tile_selfprojection_pa_t_kernel(
         y_grouped = {}
         y_codes = {}
         y_scales = {}
-        column_sums = {}
+        column_sums = [[] for batch in range(BATCH)]
         z_psum = {}
 
         def transpose_block(block, chores):
@@ -203,7 +212,7 @@ def tile_selfprojection_pa_t_kernel(
 
         def round_y(block):
             y_grouped[block] = stage.tile([P, P, PACK], BF16, name="y_rounded", align_bytes=64)
-            if block % 2:
+            if block % 2 or block == BLOCKS - 2:
                 nc.scalar.copy(out=y_grouped[block][:], in_=y_by_column[block])
             else:
                 nc.vector.tensor_copy(out=y_grouped[block][:], in_=y_by_column[block])
@@ -211,15 +220,13 @@ def tile_selfprojection_pa_t_kernel(
         def sum_y(block):
             batch, row_pass = divmod(block, ROW_PASSES)
             by_column = y_by_column[block]
-            if row_pass == 0:
-                column_sums[batch] = ring.tile([P, P], F32, name="column_sums")
-                nc.vector.tensor_reduce(out=column_sums[batch][:], in_=by_column, axis=AXIS.X, op=ALU.add)
+            sums = keep.tile([P, P], F32, name="block_sums_%d" % block)
+            nc.vector.tensor_reduce(out=sums[:], in_=by_column, axis=AXIS.X, op=ALU.add)
+            if row_pass == 0 or block == BLOCKS - 1:
+                column_sums[batch].append(sums)
             else:
-                block_sums = ring.tile([P, P], F32, name="block_sums")
-                nc.vector.tensor_reduce(out=block_sums[:], in_=by_column, axis=AXIS.X, op=ALU.add)
-                nc.gpsimd.tensor_tensor(
-                    out=column_sums[batch][:], in0=column_sums[batch][:], in1=block_sums[:], op=ALU.add
-                )
+                total = column_sums[batch][0]
+                nc.vector.tensor_tensor(out=total[:], in0=total[:], in1=sums[:], op=ALU.add)
 
         def quantize_y(block):
             y_codes[block] = ring.tile([P, P], U32, name="y_codes", align_bytes=64)
@@ -244,99 +251,84 @@ def tile_selfprojection_pa_t_kernel(
                 stop=(row_pass == ROW_PASSES - 1),
             )
 
-        z_count = P * P
-        sums_psum = {}
-        z_sbuf = {}
-        row_sum = {}
-        neg_mean = {}
-        row_squares = {}
+        z_source = {}
+        z_stats = {}
         z_gained = {}
-        c_stats = {}
-        o_sum_rows = keep.tile([1, BATCH * P], F32)
+        sums_psum = {}
 
-        def stage_row_sums(batch):
-            sums_psum[batch] = sums_pool.tile([P, P + 2], F32, name="sums_psum")
-            nc.tensor.matmul(
-                out=sums_psum[batch][:, 0:P], lhsT=ones[:], rhs=column_sums[batch][:], start=True, stop=True
-            )
-            z_sbuf[batch] = ring.tile([P, P], F32, name="z_sbuf")
-            row_sum[batch] = ring.tile([P, 1], F32, name="row_sum")
-            nc.scalar.activation(
-                out=z_sbuf[batch][:], in_=z_psum[batch][:], func=ACT.Identity, accum_out=row_sum[batch][:]
-            )
+        def prepare():
+            nc.vector.tensor_scalar_add(out=bias_sum_one[:], in0=bias_sum[:], scalar1=1.0)
 
-        def stage_total(batch):
-            nc.tensor.matmul(
-                out=sums_psum[batch][:, P : P + 1], lhsT=ones[:], rhs=row_sum[batch][:], start=True, stop=True
-            )
-            six = ring.tile([1, 6], F32, name="six")
-            nc.vector.bn_stats(out=six[:], in_=sums_psum[batch][0:1, 0:P])
-            c_stats[batch] = ring.tile([1, 2], F32, name="c_stats")
-            nc.vector.bn_aggr(out=c_stats[batch][:], in_=six[:])
+        def save_z(batch):
+            z_source[batch] = ring.tile([P, P], F32, name="z_sbuf")
+            nc.scalar.copy(out=z_source[batch][:], in_=z_psum[batch][:])
 
-        def stage_centre(batch):
-            neg_mean[batch] = ring.tile([P, 1], F32, name="neg_mean")
-            nc.scalar.activation(
-                out=neg_mean[batch][:], in_=sums_psum[batch][:, P : P + 1], func=ACT.Copy, scale=-1.0 / z_count
+        def row_stats(batch):
+            six = ring.tile([P, 6], F32, name="six")
+            nc.vector.bn_stats(out=six[:], in_=z_source[batch][:])
+            z_stats[batch] = ring.tile([P, 2], F32, name="z_stats")
+            nc.vector.bn_aggr(out=z_stats[batch][:], in_=six[:])
+
+        def total_mean(batch):
+            sums_psum[batch] = sums_pool.tile([P, 3], F32, name="sums_psum")
+            mean = z_stats[batch][:, 0:1]
+            nc.tensor.matmul(out=sums_psum[batch][:, 1:2], lhsT=centre[:], rhs=mean, start=True, stop=True)
+            nc.tensor.matmul(out=sums_psum[batch][:, 0:1], lhsT=average[:], rhs=mean, start=True, stop=True)
+
+        row_spread = {}
+
+        def row_deviation(batch):
+            moved = ring.tile([P, 2], F32, name="moved")
+            nc.vector.tensor_copy(out=moved[:], in_=sums_psum[batch][:, 0:2])
+            row_spread[batch] = ring.tile([P, 1], F32, name="row_spread")
+            nc.vector.scalar_tensor_tensor(
+                out=row_spread[batch][:],
+                in0=moved[:, 1:2],
+                scalar=moved[:, 1:2],
+                in1=z_stats[batch][:, 1:2],
+                op0=ALU.mult,
+                op1=ALU.add,
             )
-            squares = ring.tile([P, P], F32, name="squares")
-            row_squares[batch] = ring.tile([P, 1], F32, name="row_squares")
-            nc.scalar.activation(
-                out=squares[:],
-                in_=z_sbuf[batch][:],
-                func=ACT.Square,
-                bias=neg_mean[batch][:],
-                accum_out=row_squares[batch][:],
-            )
-            c_spread = ring.tile([1, 1], F32, name="c_spread")
-            nc.scalar.activation(out=c_spread[:], in_=c_stats[batch][:, 1:2], func=ACT.Sqrt, scale=P / (P - 1.0))
             z_gained[batch] = ring.tile([P, P], F32, name="z_gained")
             nc.vector.scalar_tensor_tensor(
                 out=z_gained[batch][:],
-                in0=z_sbuf[batch][:],
-                scalar=neg_mean[batch][:],
+                in0=z_source[batch][:],
+                scalar=moved[:, 0:1],
                 in1=gain[:],
-                op0=ALU.add,
-                op1=ALU.mult,
-            )
-            c_gained = ring.tile([1, P], F32, name="c_gained")
-            nc.vector.scalar_tensor_tensor(
-                out=c_gained[:],
-                in0=sums_psum[batch][0:1, 0:P],
-                scalar=c_stats[batch][:, 0:1],
-                in1=gain_sum[:],
                 op0=ALU.subtract,
                 op1=ALU.mult,
             )
-            nc.vector.tensor_scalar_add(out=c_spread[:], in0=c_spread[:], scalar1=EPS)
-            nc.vector.reciprocal(out=c_spread[:], in_=c_spread[:])
-            o_sum_row = o_sum_rows[:, P * batch : P * (batch + 1)]
-            nc.vector.scalar_tensor_tensor(
-                out=o_sum_row, in0=c_gained[:], scalar=c_spread[:], in1=bias_sum[:], op0=ALU.mult, op1=ALU.add
-            )
-            nc.vector.tensor_scalar_add(out=o_sum_row, in0=o_sum_row, scalar1=1.0)
-            if batch == BATCH - 1:
-                nc.sync.dma_start(out=out_1.rearrange("(o b) j -> o (b j)", o=1), in_=o_sum_rows[:])
 
-        def stage_total_squares(batch):
+        def total_spread(batch):
             nc.tensor.matmul(
-                out=sums_psum[batch][:, P + 1 : P + 2], lhsT=ones[:], rhs=row_squares[batch][:], start=True, stop=True
+                out=sums_psum[batch][:, 2:3], lhsT=ones[:], rhs=row_spread[batch][:], start=True, stop=True
             )
 
-        def stage_finish(batch):
-            z_spread = ring.tile([P, 1], F32, name="z_spread")
+        z_spread = {}
+
+        def take_root(batch):
+            z_spread[batch] = ring.tile([P, 1], F32, name="z_spread")
             nc.scalar.activation(
-                out=z_spread[:], in_=sums_psum[batch][:, P + 1 : P + 2], func=ACT.Sqrt, scale=1.0 / (z_count - 1)
+                out=z_spread[batch][:], in_=sums_psum[batch][:, 2:3], func=ACT.Sqrt, scale=P / (P * P - 1.0)
             )
-            nc.vector.tensor_scalar_add(out=z_spread[:], in0=z_spread[:], scalar1=EPS)
-            nc.vector.reciprocal(out=z_spread[:], in_=z_spread[:])
+
+        def finish_z(batch):
+            nc.vector.tensor_scalar_add(out=z_spread[batch][:], in0=z_spread[batch][:], scalar1=EPS)
+            nc.vector.reciprocal(out=z_spread[batch][:], in_=z_spread[batch][:])
             result = ring.tile([P, P], F32, name="result")
             nc.vector.scalar_tensor_tensor(
-                out=result[:], in0=z_gained[batch][:], scalar=z_spread[:], in1=bias[:], op0=ALU.mult, op1=ALU.add
+                out=result[:], in0=z_gained[batch][:], scalar=z_spread[batch][:], in1=bias[:], op0=ALU.mult, op1=ALU.add
             )
             nc.sync.dma_start(out=out_0[batch], in_=result[:])
 
-        stages = (stage_row_sums, stage_total, stage_centre, stage_total_squares, stage_finish)
+        def collect_c(c_psum, batch, sums, first=False, last=False):
+            nc.tensor.matmul(
+                out=c_psum[:, 0, :],
+                lhsT=selector[:, P - 1 - batch : 2 * P - 1 - batch],
+                rhs=sums[:],
+                start=first,
+                stop=last,
+            )
 
         def y_step(block):
             return max(block + 2, FIRST_PROJECT + 1)
@@ -344,30 +336,83 @@ def tile_selfprojection_pa_t_kernel(
         def contract_step(block):
             return y_step(block) + (1 if block < BLOCKS - 1 else 0)
 
-        for step in range(contract_step(BLOCKS - 1) + len(stages)):
+        for step in range(BLOCKS + 2):
             chores = []
-            for block in range(BLOCKS):
-                if step == y_step(block):
-                    for chore in (round_y, quantize_y, sum_y) if block == BLOCKS - 1 else (round_y, sum_y, quantize_y):
-                        chores.append(functools.partial(chore, block))
+            late = []
             if step == 0:
                 for u in range(PAIRS):
                     for g in range(K_PASSES):
                         chores.append(functools.partial(split_halves, u, g))
+            for batch in range(BATCH - 1):
+                done = contract_step(ROW_PASSES * (batch + 1) - 1)
+                if step == done + 1:
+                    chores.append(functools.partial(row_stats, batch))
+                    late.append(functools.partial(total_mean, batch))
+                if step == done + 2:
+                    chores.append(functools.partial(row_deviation, batch))
+                    late.append(functools.partial(total_spread, batch))
+                if step == done + 3:
+                    chores.append(functools.partial(take_root, batch))
+            for block in range(BLOCKS - 1):
+                if step == y_step(block):
+                    for chore in (round_y, sum_y, quantize_y):
+                        chores.append(functools.partial(chore, block))
+            for batch in range(BATCH - 1):
+                if step == contract_step(ROW_PASSES * (batch + 1) - 1) + 3:
+                    chores.append(functools.partial(finish_z, batch))
+            if step == BLOCKS - 4:
+                chores.append(prepare)
             if step < BLOCKS:
                 transpose_block(step, chores)
                 if step == 0:
                     load_rest()
-            else:
+            elif step == BLOCKS:
                 for chore in chores:
                     chore()
+            else:
+                round_y(BLOCKS - 1)
+                quantize_y(BLOCKS - 1)
+                for chore in chores:
+                    chore()
+                c_psum = y_pool.tile([P, PACK, P], F32, name="y_psum")
+                for batch in range(BATCH):
+                    collect_c(c_psum, batch, column_sums[batch][0], first=(batch == 0))
             for block in range(BLOCKS):
                 if step == max(block + 1, FIRST_PROJECT):
                     project_block(block)
             for block in range(BLOCKS):
                 if step == contract_step(block):
                     contract_block(block)
-            for lag in reversed(range(len(stages))):
-                for batch in range(BATCH):
-                    if step == contract_step(ROW_PASSES * (batch + 1) - 1) + lag:
-                        stages[lag](batch)
+                    if block % ROW_PASSES == ROW_PASSES - 1 and block < BLOCKS - 1:
+                        save_z(block // ROW_PASSES)
+            for task in late:
+                task()
+
+        last = BATCH - 1
+        z_source[last] = z_psum[last]
+        row_stats(last)
+        total_mean(last)
+        sum_y(BLOCKS - 1)
+        row_deviation(last)
+        total_spread(last)
+        collect_c(c_psum, last, column_sums[last][1], last=True)
+        take_root(last)
+        c = c_psum[0:BATCH, 0, :]
+        c_six = ring.tile([BATCH, 6], F32, name="c_six")
+        nc.vector.bn_stats(out=c_six[:], in_=c)
+        c_stats = ring.tile([BATCH, 2], F32, name="c_stats")
+        nc.vector.bn_aggr(out=c_stats[:], in_=c_six[:])
+        finish_z(last)
+        c_spread = ring.tile([BATCH, 1], F32, name="c_spread")
+        nc.scalar.activation(out=c_spread[:], in_=c_stats[:, 1:2], func=ACT.Sqrt, scale=P / (P - 1.0))
+        c_gained = ring.tile([BATCH, P], F32, name="c_gained")
+        nc.vector.scalar_tensor_tensor(
+            out=c_gained[:], in0=c, scalar=c_stats[:, 0:1], in1=gain_sum[:], op0=ALU.subtract, op1=ALU.mult
+        )
+        nc.vector.tensor_scalar_add(out=c_spread[:], in0=c_spread[:], scalar1=EPS)
+        nc.vector.reciprocal(out=c_spread[:], in_=c_spread[:])
+        o_sum = ring.tile([BATCH, P], F32, name="o_sum")
+        nc.vector.scalar_tensor_tensor(
+            out=o_sum[:], in0=c_gained[:], scalar=c_spread[:], in1=bias_sum_one[:], op0=ALU.mult, op1=ALU.add
+        )
+        nc.sync.dma_start(out=out_1, in_=o_sum[:])

@@ -27,11 +27,9 @@ PAIRS = 2
 WORDS_PASS = K_PASS // 2
 QUADRANTS = 4
 EPS = 1e-05
-CHUNKS = K_PASSES * PAIRS
-WORDS_CHUNK = P
-HALF = P // 2
 FIRST_PROJECT = 1
-EARLY = 3
+SORTED = (0, 2)
+FIRST_SORTED = 5
 
 FLOPS = 2 * BATCH * ROWS * K * P + 2 * BATCH * ROWS * P * P
 
@@ -57,16 +55,15 @@ def tile_selfprojection_pa_t_kernel(
         x_pool = ctx.enter_context(tc.tile_pool(name="x_pool", bufs=BLOCKS))
         stage = ctx.enter_context(tc.tile_pool(name="stage", bufs=4))
         ring = ctx.enter_context(tc.tile_pool(name="ring", bufs=3))
+        sort_pool = ctx.enter_context(tc.tile_pool(name="sort_pool", bufs=6))
         flip_psum = ctx.enter_context(tc.psum_pool(name="flip_psum", bufs=4))
         y_pool = ctx.enter_context(tc.psum_pool(name="y_pool", bufs=2))
         z_pool = ctx.enter_context(tc.psum_pool(name="z_pool", bufs=1))
         sums_pool = ctx.enter_context(tc.psum_pool(name="sums_pool", bufs=1))
 
         xj_scales = keep.tile([P, K_PASSES, P], U8, align_bytes=64)
-        chunk_scales = keep.tile([P, CHUNKS, P], U8, align_bytes=64)
         xi_scales = keep.tile([P, ROW_PASSES, P], U8, align_bytes=64)
         nc.vector.memset(xj_scales[:].bitcast(I32), 0)
-        nc.vector.memset(chunk_scales[:].bitcast(I32), 0)
         nc.vector.memset(xi_scales[:].bitcast(I32), 0)
         ones = keep.tile([P, P], F32)
         nc.vector.memset(ones[:], 1.0)
@@ -108,78 +105,63 @@ def tile_selfprojection_pa_t_kernel(
                     in_=rows[4 * quadrant : 4 * quadrant + 4].bitcast(I32),
                 )
 
-        xj_codes = keep.tile([P, K_PASSES, P * PACK], U8, align_bytes=64)
-        halves = keep.tile([P, PAIRS, K_PASSES, 2, P * PACK], U8, align_bytes=64)
-        chunk_codes = keep.tile([P, CHUNKS, P * PACK], U8, align_bytes=64)
+        xj_codes = keep.tile([P, K_PASSES, P], U32, align_bytes=64)
         xi_codes = keep.tile([P, ROW_PASSES, P], U32, align_bytes=64)
         gain = keep.tile([P, P], BF16)
         bias = keep.tile([P, P], BF16)
         gain_sum = keep.tile([BATCH, P], BF16)
         bias_sum = keep.tile([BATCH, P], BF16)
         bias_sum_one = keep.tile([BATCH, P], F32)
-        nc.vector.memset(halves[:].bitcast(I32), 0)
 
-        def split_halves(u, g):
-            nc.vector.tensor_copy(
-                out=halves[:, u, g].rearrange("p h (n t) -> p n h t", t=PACK)[:, :, :, 2 * u : 2 * u + 2],
-                in_=xj_codes[:, g, :].rearrange("p (n h e) -> p n h e", h=2, e=2),
-            )
-
-        load_quarter(0, 0)
+        for t in range(PACK):
+            load_quarter(0, t)
         load_codes(original_xj_y_words, xj_codes)
         load_scales(original_xj_y_scales, xj_scales)
-        for t in range(1, PACK):
-            load_quarter(0, t)
+        for block in (1, 2):
+            for t in range(PACK):
+                load_quarter(block, t)
+        load_codes(original_xi_y_words, xi_codes)
+        load_scales(original_xi_y_scales, xi_scales)
         for t in range(PACK):
-            load_quarter(1, t)
-        load_block(2)
-        rows = original_xj_y_scales.rearrange("g (h r) n -> r (g h) n", h=PAIRS)
-        for a in range(2):
-            for d in range(2):
-                nc.sync.dma_start(
-                    out=chunk_scales[2 * a + d : P : 32].bitcast(I32), in_=rows[a:8:2].bitcast(I32)
-                )
-        load_block(3)
-
-        def load_rest():
-            for u in range(PAIRS):
-                for h in range(2):
-                    nc.sync.dma_start(
-                        out=chunk_codes[h:P:2, u:CHUNKS:2, :].bitcast(I32),
-                        in_=halves[HALF * u : HALF * (u + 1), u, :, h, :].bitcast(I32),
-                    )
-            load_codes(original_xi_y_words, xi_codes)
-            load_scales(original_xi_y_scales, xi_scales)
-            load_block(4)
-            load_block(5)
-            nc.sync.dma_start(out=gain[:], in_=gamma_o)
-            nc.sync.dma_start(out=bias[:], in_=beta_o)
-            nc.sync.dma_start(out=gain_sum[:], in_=gamma_o_sum.partition_broadcast(BATCH))
-            nc.sync.dma_start(out=bias_sum[:], in_=beta_o_sum.partition_broadcast(BATCH))
-            for block in range(6, BLOCKS):
-                load_block(block)
+            load_quarter(3, t)
+        nc.sync.dma_start(out=gain[:], in_=gamma_o)
+        nc.sync.dma_start(out=bias[:], in_=beta_o)
+        nc.sync.dma_start(out=gain_sum[:], in_=gamma_o_sum.partition_broadcast(BATCH))
+        nc.sync.dma_start(out=bias_sum[:], in_=beta_o_sum.partition_broadcast(BATCH))
+        for block in range(4, BLOCKS):
+            load_block(block)
 
         x_codes = {}
         x_scales = {}
         y_by_column = {}
+        block_sums = {}
         y_grouped = {}
         y_codes = {}
         y_scales = {}
         column_sums = [[] for batch in range(BATCH)]
         z_psum = {}
 
+        x_sorted = {}
+
+        def sort_words(block, t):
+            words = x_rows[block][:, t, :].bitcast(F32).rearrange("p (g w u) -> p g u w", g=K_PASSES, u=PAIRS)
+            x_sorted[block, t] = sort_pool.tile([P, K_PASSES * PAIRS * P], F32, name="x_sorted")
+            nc.vector.tensor_copy(
+                out=x_sorted[block, t][:].rearrange("p (g u w) -> p g u w", g=K_PASSES, u=PAIRS), in_=words
+            )
+
         def transpose_block(block, chores):
             x_codes[block] = ring.tile([P, PACK, K_PASSES, P], U32, name="x_codes", align_bytes=64)
             x_scales[block] = ring.tile([P, PACK, K_PASSES, P], U8, name="x_scales", align_bytes=64)
             for t in range(PACK):
-                words = x_rows[block][:, t, :].bitcast(F32)
+                words = x_sorted[block, t][:] if (block, t) in x_sorted else x_rows[block][:, t, :].bitcast(F32)
                 flipped = flip_psum.tile([P, K_PASSES, PAIRS, P], F32, name="flipped")
                 for g in range(K_PASSES):
                     for u in range(PAIRS):
-                        if block < EARLY:
+                        if (block, t) not in x_sorted:
                             part = words[:, WORDS_PASS * g + u : WORDS_PASS * (g + 1) : PAIRS]
                         else:
-                            part = words[:, WORDS_PASS * g + WORDS_CHUNK * u : WORDS_PASS * g + WORDS_CHUNK * (u + 1)]
+                            part = words[:, WORDS_PASS * g + P * u : WORDS_PASS * g + P * (u + 1)]
                         nc.tensor.transpose(flipped[:, g, u, :], part, identity[:])
                 grouped = stage.tile([P, K_PASSES, P, PACK], BF16, name="grouped", align_bytes=64)
                 nc.scalar.copy(out=grouped[:].bitcast(F32), in_=flipped[:].rearrange("p g u r -> p g r u"))
@@ -188,31 +170,30 @@ def tile_selfprojection_pa_t_kernel(
                     scales=x_scales[block][:, t].rearrange("p g r -> p (g r)"),
                     in_=grouped[:].rearrange("p g r v -> p (g r v)"),
                 )
-                if t < 3:
-                    for chore in chores[t * len(chores) // 3 : (t + 1) * len(chores) // 3]:
-                        chore()
+                for chore in chores[t]:
+                    chore()
 
         def project_block(block):
             y_psum = y_pool.tile([P, PACK, P], F32, name="y_psum")
             y_by_column[block] = y_psum[:].rearrange("p t j -> p j t")
             for t in range(PACK):
-                codes, scales = (xj_codes, xj_scales) if block < EARLY else (chunk_codes, chunk_scales)
-                passes = K_PASSES if block < EARLY else CHUNKS
-                for i in range(passes):
-                    g = i * K_PASSES // passes
+                for g in range(K_PASSES):
                     nc.tensor.matmul_mx(
                         out=y_psum[:, t, :],
                         lhsT=x_codes[block][:, t, g, :].bitcast(FP8X4),
                         lhsT_scale=x_scales[block][:, t, g, :],
-                        rhs=codes[:, i, :].bitcast(FP8X4),
-                        rhs_scale=scales[:, i, :],
-                        start=(i == 0),
-                        stop=(i == passes - 1),
+                        rhs=xj_codes[:, g, :].bitcast(FP8X4),
+                        rhs_scale=xj_scales[:, g, :],
+                        start=(g == 0),
+                        stop=(g == K_PASSES - 1),
                     )
+
+        def scalar_rounds(block):
+            return True
 
         def round_y(block):
             y_grouped[block] = stage.tile([P, P, PACK], BF16, name="y_rounded", align_bytes=64)
-            if block % 2 or block == BLOCKS - 2:
+            if scalar_rounds(block):
                 nc.scalar.copy(out=y_grouped[block][:], in_=y_by_column[block])
             else:
                 nc.vector.tensor_copy(out=y_grouped[block][:], in_=y_by_column[block])
@@ -222,6 +203,11 @@ def tile_selfprojection_pa_t_kernel(
             by_column = y_by_column[block]
             sums = keep.tile([P, P], F32, name="block_sums_%d" % block)
             nc.vector.tensor_reduce(out=sums[:], in_=by_column, axis=AXIS.X, op=ALU.add)
+            block_sums[block] = sums
+
+        def add_y(block):
+            batch, row_pass = divmod(block, ROW_PASSES)
+            sums = block_sums[block]
             if row_pass == 0 or block == BLOCKS - 1:
                 column_sums[batch].append(sums)
             else:
@@ -263,14 +249,22 @@ def tile_selfprojection_pa_t_kernel(
             z_source[batch] = ring.tile([P, P], F32, name="z_sbuf")
             nc.scalar.copy(out=z_source[batch][:], in_=z_psum[batch][:])
 
+        z_six = {}
+
         def row_stats(batch):
-            six = ring.tile([P, 6], F32, name="six")
-            nc.vector.bn_stats(out=six[:], in_=z_source[batch][:])
+            z_six[batch] = ring.tile([P, 6], F32, name="six")
+            nc.vector.bn_stats(out=z_six[batch][:], in_=z_source[batch][:])
+
+        def row_aggregate(batch):
             z_stats[batch] = ring.tile([P, 2], F32, name="z_stats")
-            nc.vector.bn_aggr(out=z_stats[batch][:], in_=six[:])
+            nc.vector.bn_aggr(out=z_stats[batch][:], in_=z_six[batch][:])
 
         def total_mean(batch):
-            sums_psum[batch] = sums_pool.tile([P, 3], F32, name="sums_psum")
+            if batch < BATCH - 1:
+                sums_psum[batch] = sums_pool.tile([P, 3], F32, name="sums_psum")
+            else:
+                flipped = flip_psum.tile([P, K_PASSES, PAIRS, P], F32, name="flipped")
+                sums_psum[batch] = flipped[:, 0, 0, 0:3]
             mean = z_stats[batch][:, 0:1]
             nc.tensor.matmul(out=sums_psum[batch][:, 1:2], lhsT=centre[:], rhs=mean, start=True, stop=True)
             nc.tensor.matmul(out=sums_psum[batch][:, 0:1], lhsT=average[:], rhs=mean, start=True, stop=True)
@@ -278,22 +272,23 @@ def tile_selfprojection_pa_t_kernel(
         row_spread = {}
 
         def row_deviation(batch):
-            moved = ring.tile([P, 2], F32, name="moved")
-            nc.vector.tensor_copy(out=moved[:], in_=sums_psum[batch][:, 0:2])
             row_spread[batch] = ring.tile([P, 1], F32, name="row_spread")
+            deviation = sums_psum[batch][:, 1:2]
             nc.vector.scalar_tensor_tensor(
                 out=row_spread[batch][:],
-                in0=moved[:, 1:2],
-                scalar=moved[:, 1:2],
+                in0=deviation,
+                scalar=deviation,
                 in1=z_stats[batch][:, 1:2],
                 op0=ALU.mult,
                 op1=ALU.add,
             )
+
+        def gain_z(batch):
             z_gained[batch] = ring.tile([P, P], F32, name="z_gained")
             nc.vector.scalar_tensor_tensor(
                 out=z_gained[batch][:],
                 in0=z_source[batch][:],
-                scalar=moved[:, 0:1],
+                scalar=sums_psum[batch][:, 0:1],
                 in1=gain[:],
                 op0=ALU.subtract,
                 op1=ALU.mult,
@@ -312,9 +307,13 @@ def tile_selfprojection_pa_t_kernel(
                 out=z_spread[batch][:], in_=sums_psum[batch][:, 2:3], func=ACT.Sqrt, scale=P / (P * P - 1.0)
             )
 
-        def finish_z(batch):
+        def add_eps(batch):
             nc.vector.tensor_scalar_add(out=z_spread[batch][:], in0=z_spread[batch][:], scalar1=EPS)
+
+        def invert(batch):
             nc.vector.reciprocal(out=z_spread[batch][:], in_=z_spread[batch][:])
+
+        def finish_z(batch):
             result = ring.tile([P, P], F32, name="result")
             nc.vector.scalar_tensor_tensor(
                 out=result[:], in0=z_gained[batch][:], scalar=z_spread[batch][:], in1=bias[:], op0=ALU.mult, op1=ALU.add
@@ -323,7 +322,7 @@ def tile_selfprojection_pa_t_kernel(
 
         def collect_c(c_psum, batch, sums, first=False, last=False):
             nc.tensor.matmul(
-                out=c_psum[:, 0, :],
+                out=c_psum[:, 0, 0, :],
                 lhsT=selector[:, P - 1 - batch : 2 * P - 1 - batch],
                 rhs=sums[:],
                 start=first,
@@ -336,80 +335,111 @@ def tile_selfprojection_pa_t_kernel(
         def contract_step(block):
             return y_step(block) + (1 if block < BLOCKS - 1 else 0)
 
-        for step in range(BLOCKS + 2):
-            chores = []
+        for step in range(BLOCKS - 1):
+            chores = ([], [], [], [])
             late = []
-            if step == 0:
-                for u in range(PAIRS):
-                    for g in range(K_PASSES):
-                        chores.append(functools.partial(split_halves, u, g))
-            for batch in range(BATCH - 1):
+
+            def plan(where, work, item):
+                where.append(functools.partial(work, item))
+
+            for batch in range(BATCH - 2):
                 done = contract_step(ROW_PASSES * (batch + 1) - 1)
                 if step == done + 1:
-                    chores.append(functools.partial(row_stats, batch))
-                    late.append(functools.partial(total_mean, batch))
+                    plan(chores[0], row_stats, batch)
+                    plan(chores[1], row_aggregate, batch)
                 if step == done + 2:
-                    chores.append(functools.partial(row_deviation, batch))
-                    late.append(functools.partial(total_spread, batch))
+                    plan(late, total_mean, batch)
                 if step == done + 3:
-                    chores.append(functools.partial(take_root, batch))
+                    row_deviation(batch)
+                    gain_z(batch)
+                    plan(late, total_spread, batch)
+                if step == done + 4:
+                    plan(chores[0], take_root, batch)
+                    plan(chores[1], add_eps, batch)
+                    plan(chores[2], invert, batch)
+                    plan(chores[3], finish_z, batch)
             for block in range(BLOCKS - 1):
                 if step == y_step(block):
-                    for chore in (round_y, sum_y, quantize_y):
-                        chores.append(functools.partial(chore, block))
-            for batch in range(BATCH - 1):
-                if step == contract_step(ROW_PASSES * (batch + 1) - 1) + 3:
-                    chores.append(functools.partial(finish_z, batch))
+                    plan(chores[0], round_y, block)
+                    plan(chores[1], sum_y, block)
+                    plan(chores[2], add_y, block)
+                    plan(chores[2], quantize_y, block)
+            if FIRST_SORTED <= step + 2 < BLOCKS:
+                for t, slot in zip(SORTED, (1, 2)):
+                    chores[slot].append(functools.partial(sort_words, step + 2, t))
             if step == BLOCKS - 4:
-                chores.append(prepare)
-            if step < BLOCKS:
-                transpose_block(step, chores)
-                if step == 0:
-                    load_rest()
-            elif step == BLOCKS:
-                for chore in chores:
-                    chore()
-            else:
-                round_y(BLOCKS - 1)
-                quantize_y(BLOCKS - 1)
-                for chore in chores:
-                    chore()
-                c_psum = y_pool.tile([P, PACK, P], F32, name="y_psum")
-                for batch in range(BATCH):
-                    collect_c(c_psum, batch, column_sums[batch][0], first=(batch == 0))
+                chores[3].append(prepare)
+            transpose_block(step, chores)
+            for task in late:
+                task()
             for block in range(BLOCKS):
                 if step == max(block + 1, FIRST_PROJECT):
                     project_block(block)
             for block in range(BLOCKS):
                 if step == contract_step(block):
                     contract_block(block)
-                    if block % ROW_PASSES == ROW_PASSES - 1 and block < BLOCKS - 1:
+                    if block % ROW_PASSES == ROW_PASSES - 1:
                         save_z(block // ROW_PASSES)
-            for task in late:
-                task()
 
-        last = BATCH - 1
+        third, last = BATCH - 2, BATCH - 1
+        final = BLOCKS - 1
+        sum_y(final - 2)
+        transpose_block(final, ([], [functools.partial(round_y, final - 2)], [], []))
+        project_block(final - 1)
+        contract_block(final - 3)
+        project_block(final)
+        quantize_y(final - 2)
+        contract_block(final - 2)
+        c_psum = flip_psum.tile([P, K_PASSES, PAIRS, P], F32, name="flipped")
+        for batch in range(2):
+            collect_c(c_psum, batch, column_sums[batch][0], first=(batch == 0))
+        round_y(final - 1)
+        row_stats(third)
+        add_y(final - 2)
+        sum_y(final - 1)
+        row_aggregate(third)
+        quantize_y(final - 1)
+        contract_block(final - 1)
+        add_y(final - 1)
+        round_y(final)
+        quantize_y(final)
+        total_mean(third)
+        contract_block(final)
+        for batch in range(2, BATCH):
+            collect_c(c_psum, batch, column_sums[batch][0])
+        sum_y(final)
+        add_y(final)
         z_source[last] = z_psum[last]
         row_stats(last)
+        row_deviation(third)
+        row_aggregate(last)
+        gain_z(third)
         total_mean(last)
-        sum_y(BLOCKS - 1)
-        row_deviation(last)
-        total_spread(last)
+        total_spread(third)
+        take_root(third)
         collect_c(c_psum, last, column_sums[last][1], last=True)
-        take_root(last)
-        c = c_psum[0:BATCH, 0, :]
+        row_deviation(last)
+        gain_z(last)
+        total_spread(last)
+        add_eps(third)
+        c = c_psum[0:BATCH, 0, 0, :]
         c_six = ring.tile([BATCH, 6], F32, name="c_six")
         nc.vector.bn_stats(out=c_six[:], in_=c)
+        invert(third)
+        take_root(last)
         c_stats = ring.tile([BATCH, 2], F32, name="c_stats")
         nc.vector.bn_aggr(out=c_stats[:], in_=c_six[:])
-        finish_z(last)
+        add_eps(last)
+        finish_z(third)
         c_spread = ring.tile([BATCH, 1], F32, name="c_spread")
         nc.scalar.activation(out=c_spread[:], in_=c_stats[:, 1:2], func=ACT.Sqrt, scale=P / (P - 1.0))
         c_gained = ring.tile([BATCH, P], F32, name="c_gained")
         nc.vector.scalar_tensor_tensor(
             out=c_gained[:], in0=c, scalar=c_stats[:, 0:1], in1=gain_sum[:], op0=ALU.subtract, op1=ALU.mult
         )
+        invert(last)
         nc.vector.tensor_scalar_add(out=c_spread[:], in0=c_spread[:], scalar1=EPS)
+        finish_z(last)
         nc.vector.reciprocal(out=c_spread[:], in_=c_spread[:])
         o_sum = ring.tile([BATCH, P], F32, name="o_sum")
         nc.vector.scalar_tensor_tensor(

@@ -28,8 +28,6 @@ WORDS_PASS = K_PASS // 2
 QUADRANTS = 4
 EPS = 1e-05
 FIRST_PROJECT = 1
-SORTED = (0, 2)
-FIRST_SORTED = 5
 
 FLOPS = 2 * BATCH * ROWS * K * P + 2 * BATCH * ROWS * P * P
 
@@ -55,7 +53,6 @@ def tile_selfprojection_pa_t_kernel(
         x_pool = ctx.enter_context(tc.tile_pool(name="x_pool", bufs=BLOCKS))
         stage = ctx.enter_context(tc.tile_pool(name="stage", bufs=4))
         ring = ctx.enter_context(tc.tile_pool(name="ring", bufs=3))
-        sort_pool = ctx.enter_context(tc.tile_pool(name="sort_pool", bufs=6))
         flip_psum = ctx.enter_context(tc.psum_pool(name="flip_psum", bufs=4))
         y_pool = ctx.enter_context(tc.psum_pool(name="y_pool", bufs=2))
         z_pool = ctx.enter_context(tc.psum_pool(name="z_pool", bufs=1))
@@ -75,10 +72,8 @@ def tile_selfprojection_pa_t_kernel(
         nc.scalar.activation(out=warm[:], in_=warm[:], func=ACT.Sqrt)
         identity = keep.tile([P, P], F32)
         make_identity(nc, identity[:])
-        average = keep.tile([P, P], F32)
-        nc.vector.memset(average[:], 1.0 / P)
         centre = keep.tile([P, P], F32)
-        nc.vector.tensor_tensor(out=centre[:], in0=identity[:], in1=average[:], op=ALU.subtract)
+        nc.vector.tensor_scalar_add(out=centre[:], in0=identity[:], scalar1=-1.0 / P)
 
         x_blocks_hbm = x.rearrange("b (g p t) k -> (b g) p t k", p=P, t=PACK)
         x_rows = []
@@ -141,27 +136,15 @@ def tile_selfprojection_pa_t_kernel(
         column_sums = [[] for batch in range(BATCH)]
         z_psum = {}
 
-        x_sorted = {}
-
-        def sort_words(block, t):
-            words = x_rows[block][:, t, :].bitcast(F32).rearrange("p (g w u) -> p g u w", g=K_PASSES, u=PAIRS)
-            x_sorted[block, t] = sort_pool.tile([P, K_PASSES * PAIRS * P], F32, name="x_sorted")
-            nc.vector.tensor_copy(
-                out=x_sorted[block, t][:].rearrange("p (g u w) -> p g u w", g=K_PASSES, u=PAIRS), in_=words
-            )
-
         def transpose_block(block, chores):
             x_codes[block] = ring.tile([P, PACK, K_PASSES, P], U32, name="x_codes", align_bytes=64)
             x_scales[block] = ring.tile([P, PACK, K_PASSES, P], U8, name="x_scales", align_bytes=64)
             for t in range(PACK):
-                words = x_sorted[block, t][:] if (block, t) in x_sorted else x_rows[block][:, t, :].bitcast(F32)
+                words = x_rows[block][:, t, :].bitcast(F32)
                 flipped = flip_psum.tile([P, K_PASSES, PAIRS, P], F32, name="flipped")
                 for g in range(K_PASSES):
                     for u in range(PAIRS):
-                        if (block, t) not in x_sorted:
-                            part = words[:, WORDS_PASS * g + u : WORDS_PASS * (g + 1) : PAIRS]
-                        else:
-                            part = words[:, WORDS_PASS * g + P * u : WORDS_PASS * g + P * (u + 1)]
+                        part = words[:, WORDS_PASS * g + u : WORDS_PASS * (g + 1) : PAIRS]
                         nc.tensor.transpose(flipped[:, g, u, :], part, identity[:])
                 grouped = stage.tile([P, K_PASSES, P, PACK], BF16, name="grouped", align_bytes=64)
                 nc.scalar.copy(out=grouped[:].bitcast(F32), in_=flipped[:].rearrange("p g u r -> p g r u"))
@@ -189,7 +172,7 @@ def tile_selfprojection_pa_t_kernel(
                     )
 
         def scalar_rounds(block):
-            return True
+            return block % 2 == 1 or block >= BLOCKS - 3
 
         def round_y(block):
             y_grouped[block] = stage.tile([P, P, PACK], BF16, name="y_rounded", align_bytes=64)
@@ -259,21 +242,22 @@ def tile_selfprojection_pa_t_kernel(
             z_stats[batch] = ring.tile([P, 2], F32, name="z_stats")
             nc.vector.bn_aggr(out=z_stats[batch][:], in_=z_six[batch][:])
 
-        def total_mean(batch):
+        def centre_means(batch):
             if batch < BATCH - 1:
-                sums_psum[batch] = sums_pool.tile([P, 3], F32, name="sums_psum")
+                sums_psum[batch] = sums_pool.tile([P, 2 + P], F32, name="sums_psum")
             else:
                 flipped = flip_psum.tile([P, K_PASSES, PAIRS, P], F32, name="flipped")
-                sums_psum[batch] = flipped[:, 0, 0, 0:3]
-            mean = z_stats[batch][:, 0:1]
-            nc.tensor.matmul(out=sums_psum[batch][:, 1:2], lhsT=centre[:], rhs=mean, start=True, stop=True)
-            nc.tensor.matmul(out=sums_psum[batch][:, 0:1], lhsT=average[:], rhs=mean, start=True, stop=True)
+                sums_psum[batch] = flipped[:, 0].rearrange("p u r -> p (u r)")
+            nc.tensor.matmul(
+                out=sums_psum[batch][:, 0:1], lhsT=centre[:], rhs=z_stats[batch][:, 0:1], start=True, stop=True
+            )
 
         row_spread = {}
+        z_mean = {}
 
         def row_deviation(batch):
             row_spread[batch] = ring.tile([P, 1], F32, name="row_spread")
-            deviation = sums_psum[batch][:, 1:2]
+            deviation = sums_psum[batch][:, 0:1]
             nc.vector.scalar_tensor_tensor(
                 out=row_spread[batch][:],
                 in0=deviation,
@@ -282,13 +266,17 @@ def tile_selfprojection_pa_t_kernel(
                 op0=ALU.mult,
                 op1=ALU.add,
             )
+            z_mean[batch] = ring.tile([P, 1], F32, name="z_mean")
+            nc.vector.tensor_tensor(
+                out=z_mean[batch][:], in0=z_stats[batch][:, 0:1], in1=deviation, op=ALU.subtract
+            )
 
         def gain_z(batch):
             z_gained[batch] = ring.tile([P, P], F32, name="z_gained")
             nc.vector.scalar_tensor_tensor(
                 out=z_gained[batch][:],
                 in0=z_source[batch][:],
-                scalar=sums_psum[batch][:, 0:1],
+                scalar=z_mean[batch][:],
                 in1=gain[:],
                 op0=ALU.subtract,
                 op1=ALU.mult,
@@ -296,7 +284,7 @@ def tile_selfprojection_pa_t_kernel(
 
         def total_spread(batch):
             nc.tensor.matmul(
-                out=sums_psum[batch][:, 2:3], lhsT=ones[:], rhs=row_spread[batch][:], start=True, stop=True
+                out=sums_psum[batch][:, 1:2], lhsT=ones[:], rhs=row_spread[batch][:], start=True, stop=True
             )
 
         z_spread = {}
@@ -304,7 +292,7 @@ def tile_selfprojection_pa_t_kernel(
         def take_root(batch):
             z_spread[batch] = ring.tile([P, 1], F32, name="z_spread")
             nc.scalar.activation(
-                out=z_spread[batch][:], in_=sums_psum[batch][:, 2:3], func=ACT.Sqrt, scale=P / (P * P - 1.0)
+                out=z_spread[batch][:], in_=sums_psum[batch][:, 1:2], func=ACT.Sqrt, scale=P / (P * P - 1.0)
             )
 
         def add_eps(batch):
@@ -320,14 +308,22 @@ def tile_selfprojection_pa_t_kernel(
             )
             nc.sync.dma_start(out=out_0[batch], in_=result[:])
 
-        def collect_c(c_psum, batch, sums, first=False, last=False):
+        def collect_c(out, batch, sums, first=True, last=True):
             nc.tensor.matmul(
-                out=c_psum[:, 0, 0, :],
-                lhsT=selector[:, P - 1 - batch : 2 * P - 1 - batch],
-                rhs=sums[:],
-                start=first,
-                stop=last,
+                out=out, lhsT=selector[:, P - 1 - batch : 2 * P - 1 - batch], rhs=sums[:], start=first, stop=last
             )
+
+        c_early = keep.tile([BATCH, P], F32)
+
+        def collect_early(batch):
+            collect_c(sums_psum[batch][:, 2 : 2 + P], batch, column_sums[batch][0])
+
+        def keep_early(batch):
+            c = sums_psum[batch][0:BATCH, 2 : 2 + P]
+            if batch == 0:
+                nc.vector.tensor_copy(out=c_early[:], in_=c)
+            else:
+                nc.vector.tensor_tensor(out=c_early[:], in0=c, in1=c_early[:], op=ALU.add)
 
         def y_step(block):
             return max(block + 2, FIRST_PROJECT + 1)
@@ -348,9 +344,11 @@ def tile_selfprojection_pa_t_kernel(
                     plan(chores[0], row_stats, batch)
                     plan(chores[1], row_aggregate, batch)
                 if step == done + 2:
-                    plan(late, total_mean, batch)
+                    plan(late, centre_means, batch)
+                    plan(late, collect_early, batch)
                 if step == done + 3:
                     row_deviation(batch)
+                    keep_early(batch)
                     gain_z(batch)
                     plan(late, total_spread, batch)
                 if step == done + 4:
@@ -364,9 +362,6 @@ def tile_selfprojection_pa_t_kernel(
                     plan(chores[1], sum_y, block)
                     plan(chores[2], add_y, block)
                     plan(chores[2], quantize_y, block)
-            if FIRST_SORTED <= step + 2 < BLOCKS:
-                for t, slot in zip(SORTED, (1, 2)):
-                    chores[slot].append(functools.partial(sort_words, step + 2, t))
             if step == BLOCKS - 4:
                 chores[3].append(prepare)
             transpose_block(step, chores)
@@ -390,9 +385,6 @@ def tile_selfprojection_pa_t_kernel(
         project_block(final)
         quantize_y(final - 2)
         contract_block(final - 2)
-        c_psum = flip_psum.tile([P, K_PASSES, PAIRS, P], F32, name="flipped")
-        for batch in range(2):
-            collect_c(c_psum, batch, column_sums[batch][0], first=(batch == 0))
         round_y(final - 1)
         row_stats(third)
         add_y(final - 2)
@@ -403,10 +395,11 @@ def tile_selfprojection_pa_t_kernel(
         add_y(final - 1)
         round_y(final)
         quantize_y(final)
-        total_mean(third)
+        centre_means(third)
         contract_block(final)
-        for batch in range(2, BATCH):
-            collect_c(c_psum, batch, column_sums[batch][0])
+        c_psum = flip_psum.tile([P, K_PASSES, PAIRS, P], F32, name="flipped")
+        collect_c(c_psum[:, 0, 0, :], third, column_sums[third][0], last=False)
+        collect_c(c_psum[:, 0, 0, :], last, column_sums[last][0], first=False, last=False)
         sum_y(final)
         add_y(final)
         z_source[last] = z_psum[last]
@@ -414,17 +407,18 @@ def tile_selfprojection_pa_t_kernel(
         row_deviation(third)
         row_aggregate(last)
         gain_z(third)
-        total_mean(last)
+        centre_means(last)
         total_spread(third)
         take_root(third)
-        collect_c(c_psum, last, column_sums[last][1], last=True)
+        collect_c(c_psum[:, 0, 0, :], last, column_sums[last][1], first=False)
         row_deviation(last)
         gain_z(last)
         total_spread(last)
         add_eps(third)
-        c = c_psum[0:BATCH, 0, 0, :]
+        c = keep.tile([BATCH, P], F32)
+        nc.vector.tensor_tensor(out=c[:], in0=c_psum[0:BATCH, 0, 0, :], in1=c_early[:], op=ALU.add)
         c_six = ring.tile([BATCH, 6], F32, name="c_six")
-        nc.vector.bn_stats(out=c_six[:], in_=c)
+        nc.vector.bn_stats(out=c_six[:], in_=c[:])
         invert(third)
         take_root(last)
         c_stats = ring.tile([BATCH, 2], F32, name="c_stats")
@@ -435,7 +429,7 @@ def tile_selfprojection_pa_t_kernel(
         nc.scalar.activation(out=c_spread[:], in_=c_stats[:, 1:2], func=ACT.Sqrt, scale=P / (P - 1.0))
         c_gained = ring.tile([BATCH, P], F32, name="c_gained")
         nc.vector.scalar_tensor_tensor(
-            out=c_gained[:], in0=c, scalar=c_stats[:, 0:1], in1=gain_sum[:], op0=ALU.subtract, op1=ALU.mult
+            out=c_gained[:], in0=c[:], scalar=c_stats[:, 0:1], in1=gain_sum[:], op0=ALU.subtract, op1=ALU.mult
         )
         invert(last)
         nc.vector.tensor_scalar_add(out=c_spread[:], in0=c_spread[:], scalar1=EPS)

@@ -27,7 +27,6 @@ PAIRS = 2
 WORDS_PASS = K_PASS // 2
 QUADRANTS = 4
 EPS = 1e-05
-FIRST_PROJECT = 1
 
 FLOPS = 2 * BATCH * ROWS * K * P + 2 * BATCH * ROWS * P * P
 
@@ -62,18 +61,16 @@ def tile_selfprojection_pa_t_kernel(
         xi_scales = keep.tile([P, ROW_PASSES, P], U8, align_bytes=64)
         nc.vector.memset(xj_scales[:].bitcast(I32), 0)
         nc.vector.memset(xi_scales[:].bitcast(I32), 0)
-        ones = keep.tile([P, P], F32)
-        nc.vector.memset(ones[:], 1.0)
-        selector = keep.tile([P, 2 * P - 1], F32)
+        selector = keep.tile([P, P], F32)
         nc.vector.memset(selector[:], 0.0)
-        nc.vector.memset(selector[:, P - 1 : P], 1.0)
+        nc.vector.memset(selector[:, BATCH - 1 : BATCH], 1.0)
         warm = keep.tile([P, 1], F32)
         nc.vector.memset(warm[:], 1.0)
         nc.scalar.activation(out=warm[:], in_=warm[:], func=ACT.Sqrt)
         identity = keep.tile([P, P], F32)
         make_identity(nc, identity[:])
-        centre = keep.tile([P, P], F32)
-        nc.vector.tensor_scalar_add(out=centre[:], in0=identity[:], scalar1=-1.0 / P)
+        c_columns = keep.tile([P, P], F32)
+        nc.vector.memset(c_columns[:], 0.0)
 
         x_blocks_hbm = x.rearrange("b (g p t) k -> (b g) p t k", p=P, t=PACK)
         x_rows = []
@@ -172,7 +169,7 @@ def tile_selfprojection_pa_t_kernel(
                     )
 
         def scalar_rounds(block):
-            return block % 2 == 1 or block >= BLOCKS - 3
+            return block % 4 != 0 or block >= BLOCKS - 3
 
         def round_y(block):
             y_grouped[block] = stage.tile([P, P, PACK], BF16, name="y_rounded", align_bytes=64)
@@ -191,7 +188,7 @@ def tile_selfprojection_pa_t_kernel(
         def add_y(block):
             batch, row_pass = divmod(block, ROW_PASSES)
             sums = block_sums[block]
-            if row_pass == 0 or block == BLOCKS - 1:
+            if row_pass == 0:
                 column_sums[batch].append(sums)
             else:
                 total = column_sums[batch][0]
@@ -221,54 +218,78 @@ def tile_selfprojection_pa_t_kernel(
             )
 
         z_source = {}
+        z_six = {}
         z_stats = {}
+        spread_psum = {}
+        mean_six = {}
+        mean_stats = {}
+        variance_sum = {}
+        z_spread = {}
         z_gained = {}
-        sums_psum = {}
-
-        def prepare():
-            nc.vector.tensor_scalar_add(out=bias_sum_one[:], in0=bias_sum[:], scalar1=1.0)
 
         def save_z(batch):
             z_source[batch] = ring.tile([P, P], F32, name="z_sbuf")
             nc.scalar.copy(out=z_source[batch][:], in_=z_psum[batch][:])
 
-        z_six = {}
-
         def row_stats(batch):
-            z_six[batch] = ring.tile([P, 6], F32, name="six")
+            z_six[batch] = ring.tile([P, 6], F32, name="z_six")
             nc.vector.bn_stats(out=z_six[batch][:], in_=z_source[batch][:])
 
         def row_aggregate(batch):
             z_stats[batch] = ring.tile([P, 2], F32, name="z_stats")
             nc.vector.bn_aggr(out=z_stats[batch][:], in_=z_six[batch][:])
 
-        def centre_means(batch):
+        def spread_rows(batch):
             if batch < BATCH - 1:
-                sums_psum[batch] = sums_pool.tile([P, 2 + P], F32, name="sums_psum")
+                spread_psum[batch] = sums_pool.tile([P, 3, P], F32, name="sums_psum")
             else:
                 flipped = flip_psum.tile([P, K_PASSES, PAIRS, P], F32, name="flipped")
-                sums_psum[batch] = flipped[:, 0].rearrange("p u r -> p (u r)")
-            nc.tensor.matmul(
-                out=sums_psum[batch][:, 0:1], lhsT=centre[:], rhs=z_stats[batch][:, 0:1], start=True, stop=True
+                spread_psum[batch] = flipped[:].rearrange("p g u r -> p (g u) r")
+            for i in range(2):
+                nc.tensor.transpose(
+                    spread_psum[batch][:, i, :], z_stats[batch][:, i : i + 1].to_broadcast([P, P]), identity[:]
+                )
+            if batch < BATCH - 1:
+                nc.tensor.transpose(spread_psum[batch][:, 2, :], column_sums[batch][0][:], identity[:])
+
+        def sum_c(batch):
+            scratch = ring.tile([P, P], F32, name="scratch")
+            nc.scalar.activation(
+                out=scratch[:],
+                in_=spread_psum[batch][:, 2, :],
+                func=ACT.Copy,
+                accum_out=c_columns[:, batch : batch + 1],
             )
 
-        row_spread = {}
-        z_mean = {}
+        def sum_variances(batch):
+            scratch = ring.tile([P, P], F32, name="scratch")
+            variance_sum[batch] = ring.tile([P, 1], F32, name="variance_sum")
+            nc.scalar.activation(
+                out=scratch[:], in_=spread_psum[batch][:, 1, :], func=ACT.Copy, accum_out=variance_sum[batch][:]
+            )
 
-        def row_deviation(batch):
-            row_spread[batch] = ring.tile([P, 1], F32, name="row_spread")
-            deviation = sums_psum[batch][:, 0:1]
+        def mean_row_stats(batch):
+            mean_six[batch] = ring.tile([P, 6], F32, name="mean_six")
+            nc.vector.bn_stats(out=mean_six[batch][:], in_=spread_psum[batch][:, 0, :])
+
+        def mean_row_aggregate(batch):
+            mean_stats[batch] = ring.tile([P, 2], F32, name="mean_stats")
+            nc.vector.bn_aggr(out=mean_stats[batch][:], in_=mean_six[batch][:])
+
+        def total_variance(batch):
+            z_spread[batch] = ring.tile([P, 1], F32, name="z_spread")
             nc.vector.scalar_tensor_tensor(
-                out=row_spread[batch][:],
-                in0=deviation,
-                scalar=deviation,
-                in1=z_stats[batch][:, 1:2],
+                out=z_spread[batch][:],
+                in0=variance_sum[batch][:],
+                scalar=1.0 / P,
+                in1=mean_stats[batch][:, 1:2],
                 op0=ALU.mult,
                 op1=ALU.add,
             )
-            z_mean[batch] = ring.tile([P, 1], F32, name="z_mean")
-            nc.vector.tensor_tensor(
-                out=z_mean[batch][:], in0=z_stats[batch][:, 0:1], in1=deviation, op=ALU.subtract
+
+        def take_root(batch):
+            nc.scalar.activation(
+                out=z_spread[batch][:], in_=z_spread[batch][:], func=ACT.Sqrt, scale=P * P / (P * P - 1.0)
             )
 
         def gain_z(batch):
@@ -276,23 +297,10 @@ def tile_selfprojection_pa_t_kernel(
             nc.vector.scalar_tensor_tensor(
                 out=z_gained[batch][:],
                 in0=z_source[batch][:],
-                scalar=z_mean[batch][:],
+                scalar=mean_stats[batch][:, 0:1],
                 in1=gain[:],
                 op0=ALU.subtract,
                 op1=ALU.mult,
-            )
-
-        def total_spread(batch):
-            nc.tensor.matmul(
-                out=sums_psum[batch][:, 1:2], lhsT=ones[:], rhs=row_spread[batch][:], start=True, stop=True
-            )
-
-        z_spread = {}
-
-        def take_root(batch):
-            z_spread[batch] = ring.tile([P, 1], F32, name="z_spread")
-            nc.scalar.activation(
-                out=z_spread[batch][:], in_=sums_psum[batch][:, 1:2], func=ACT.Sqrt, scale=P / (P * P - 1.0)
             )
 
         def add_eps(batch):
@@ -308,132 +316,118 @@ def tile_selfprojection_pa_t_kernel(
             )
             nc.sync.dma_start(out=out_0[batch], in_=result[:])
 
-        def collect_c(out, batch, sums, first=True, last=True):
-            nc.tensor.matmul(
-                out=out, lhsT=selector[:, P - 1 - batch : 2 * P - 1 - batch], rhs=sums[:], start=first, stop=last
-            )
+        def prepare():
+            nc.vector.tensor_scalar_add(out=bias_sum_one[:], in0=bias_sum[:], scalar1=1.0)
 
-        c_early = keep.tile([BATCH, P], F32)
+        def plan(where, work, item):
+            where.append(functools.partial(work, item))
 
-        def collect_early(batch):
-            collect_c(sums_psum[batch][:, 2 : 2 + P], batch, column_sums[batch][0])
-
-        def keep_early(batch):
-            c = sums_psum[batch][0:BATCH, 2 : 2 + P]
-            if batch == 0:
-                nc.vector.tensor_copy(out=c_early[:], in_=c)
-            else:
-                nc.vector.tensor_tensor(out=c_early[:], in0=c, in1=c_early[:], op=ALU.add)
-
-        def y_step(block):
-            return max(block + 2, FIRST_PROJECT + 1)
-
-        def contract_step(block):
-            return y_step(block) + (1 if block < BLOCKS - 1 else 0)
-
-        for step in range(BLOCKS - 1):
+        for step in range(BLOCKS):
             chores = ([], [], [], [])
             late = []
-
-            def plan(where, work, item):
-                where.append(functools.partial(work, item))
-
             for batch in range(BATCH - 2):
-                done = contract_step(ROW_PASSES * (batch + 1) - 1)
+                done = ROW_PASSES * (batch + 1) + 2
                 if step == done + 1:
                     plan(chores[0], row_stats, batch)
                     plan(chores[1], row_aggregate, batch)
                 if step == done + 2:
-                    plan(late, centre_means, batch)
-                    plan(late, collect_early, batch)
+                    plan(late, spread_rows, batch)
                 if step == done + 3:
-                    row_deviation(batch)
-                    keep_early(batch)
-                    gain_z(batch)
-                    plan(late, total_spread, batch)
+                    plan(chores[0], sum_variances, batch)
+                    plan(chores[0], mean_row_stats, batch)
+                    plan(chores[1], sum_c, batch)
+                    plan(chores[1], mean_row_aggregate, batch)
+                    plan(chores[2], total_variance, batch)
+                    plan(chores[3], take_root, batch)
                 if step == done + 4:
-                    plan(chores[0], take_root, batch)
+                    plan(chores[0], gain_z, batch)
                     plan(chores[1], add_eps, batch)
                     plan(chores[2], invert, batch)
                     plan(chores[3], finish_z, batch)
-            for block in range(BLOCKS - 1):
-                if step == y_step(block):
-                    plan(chores[0], round_y, block)
-                    plan(chores[1], sum_y, block)
-                    plan(chores[2], add_y, block)
-                    plan(chores[2], quantize_y, block)
+            block = step - 2
+            if 0 <= block < BLOCKS - 3:
+                plan(chores[0], round_y, block)
+                plan(chores[1], sum_y, block)
+                plan(chores[2], quantize_y, block)
+                plan(chores[2], add_y, block)
+            if step == BLOCKS - 1:
+                round_y(block)
+                sum_y(block)
             if step == BLOCKS - 4:
                 chores[3].append(prepare)
             transpose_block(step, chores)
             for task in late:
                 task()
-            for block in range(BLOCKS):
-                if step == max(block + 1, FIRST_PROJECT):
-                    project_block(block)
-            for block in range(BLOCKS):
-                if step == contract_step(block):
-                    contract_block(block)
-                    if block % ROW_PASSES == ROW_PASSES - 1:
-                        save_z(block // ROW_PASSES)
+            if step >= 3:
+                contract_block(step - 3)
+                if step % ROW_PASSES == 2:
+                    save_z((step - 3) // ROW_PASSES)
+            if step >= 1:
+                project_block(step - 1)
 
         third, last = BATCH - 2, BATCH - 1
         final = BLOCKS - 1
-        sum_y(final - 2)
-        transpose_block(final, ([], [functools.partial(round_y, final - 2)], [], []))
-        project_block(final - 1)
-        contract_block(final - 3)
-        project_block(final)
         quantize_y(final - 2)
+        project_block(final)
         contract_block(final - 2)
-        round_y(final - 1)
         row_stats(third)
-        add_y(final - 2)
+        round_y(final - 1)
         sum_y(final - 1)
         row_aggregate(third)
         quantize_y(final - 1)
+        spread_rows(third)
         contract_block(final - 1)
-        add_y(final - 1)
         round_y(final)
         quantize_y(final)
-        centre_means(third)
         contract_block(final)
-        c_psum = flip_psum.tile([P, K_PASSES, PAIRS, P], F32, name="flipped")
-        collect_c(c_psum[:, 0, 0, :], third, column_sums[third][0], last=False)
-        collect_c(c_psum[:, 0, 0, :], last, column_sums[last][0], first=False, last=False)
+        sum_variances(third)
+        sum_c(third)
         sum_y(final)
-        add_y(final)
         z_source[last] = z_psum[last]
         row_stats(last)
-        row_deviation(third)
+        add_y(final - 2)
         row_aggregate(last)
-        gain_z(third)
-        centre_means(last)
-        total_spread(third)
+        add_y(final - 1)
+        c_early_psum = flip_psum.tile([P, K_PASSES, PAIRS, P], F32, name="flipped")
+        nc.tensor.transpose(c_early_psum[:, 0, 0, :], c_columns[:], identity[:])
+        spread_rows(last)
+        c_early = keep.tile([BATCH, P], F32)
+        nc.scalar.copy(out=c_early[:], in_=c_early_psum[0:BATCH, 0, 0, :])
+        mean_row_stats(third)
+        add_y(final)
+        sum_variances(last)
+        c_psum = flip_psum.tile([P, K_PASSES, PAIRS, P], F32, name="flipped")
+        nc.tensor.matmul(
+            out=c_psum[:, 0, 0, :], lhsT=selector[:], rhs=column_sums[last][0][:], start=True, stop=True
+        )
+        mean_row_aggregate(third)
+        mean_row_stats(last)
+        total_variance(third)
         take_root(third)
-        collect_c(c_psum[:, 0, 0, :], last, column_sums[last][1], first=False)
-        row_deviation(last)
+        mean_row_aggregate(last)
+        gain_z(third)
+        total_variance(last)
+        take_root(last)
         gain_z(last)
-        total_spread(last)
         add_eps(third)
+        add_eps(last)
         c = keep.tile([BATCH, P], F32)
         nc.vector.tensor_tensor(out=c[:], in0=c_psum[0:BATCH, 0, 0, :], in1=c_early[:], op=ALU.add)
+        invert(third)
+        invert(last)
         c_six = ring.tile([BATCH, 6], F32, name="c_six")
         nc.vector.bn_stats(out=c_six[:], in_=c[:])
-        invert(third)
-        take_root(last)
+        finish_z(last)
         c_stats = ring.tile([BATCH, 2], F32, name="c_stats")
         nc.vector.bn_aggr(out=c_stats[:], in_=c_six[:])
-        add_eps(last)
-        finish_z(third)
         c_spread = ring.tile([BATCH, 1], F32, name="c_spread")
         nc.scalar.activation(out=c_spread[:], in_=c_stats[:, 1:2], func=ACT.Sqrt, scale=P / (P - 1.0))
+        finish_z(third)
         c_gained = ring.tile([BATCH, P], F32, name="c_gained")
         nc.vector.scalar_tensor_tensor(
             out=c_gained[:], in0=c[:], scalar=c_stats[:, 0:1], in1=gain_sum[:], op0=ALU.subtract, op1=ALU.mult
         )
-        invert(last)
         nc.vector.tensor_scalar_add(out=c_spread[:], in0=c_spread[:], scalar1=EPS)
-        finish_z(last)
         nc.vector.reciprocal(out=c_spread[:], in_=c_spread[:])
         o_sum = ring.tile([BATCH, P], F32, name="o_sum")
         nc.vector.scalar_tensor_tensor(

@@ -52,6 +52,7 @@ def tile_selfprojection_pa_t_kernel(
         x_pool = ctx.enter_context(tc.tile_pool(name="x_pool", bufs=BLOCKS))
         stage = ctx.enter_context(tc.tile_pool(name="stage", bufs=4))
         ring = ctx.enter_context(tc.tile_pool(name="ring", bufs=3))
+        sort_pool = ctx.enter_context(tc.tile_pool(name="sort_pool", bufs=6))
         flip_psum = ctx.enter_context(tc.psum_pool(name="flip_psum", bufs=4))
         y_pool = ctx.enter_context(tc.psum_pool(name="y_pool", bufs=2))
         z_pool = ctx.enter_context(tc.psum_pool(name="z_pool", bufs=1))
@@ -77,8 +78,8 @@ def tile_selfprojection_pa_t_kernel(
         for block in range(BLOCKS):
             x_rows.append(x_pool.tile([P, PACK, K], BF16, name="x_rows"))
 
-        def load_quarter(block, t):
-            nc.sync.dma_start(out=x_rows[block][:, t, :], in_=x_blocks_hbm[block, :, t, :])
+        def load_quarters(block, first, end):
+            nc.sync.dma_start(out=x_rows[block][:, first:end, :], in_=x_blocks_hbm[block, :, first:end, :])
 
         def load_block(block):
             nc.sync.dma_start(out=x_rows[block][:], in_=x_blocks_hbm[block])
@@ -105,17 +106,18 @@ def tile_selfprojection_pa_t_kernel(
         bias_sum = keep.tile([BATCH, P], BF16)
         bias_sum_one = keep.tile([BATCH, P], F32)
 
-        for t in range(PACK):
-            load_quarter(0, t)
+        load_quarters(0, 0, 1)
+        load_quarters(0, 1, 2)
+        load_quarters(0, 2, 4)
         load_codes(original_xj_y_words, xj_codes)
         load_scales(original_xj_y_scales, xj_scales)
         for block in (1, 2):
-            for t in range(PACK):
-                load_quarter(block, t)
+            load_quarters(block, 0, 2)
+            load_quarters(block, 2, 4)
         load_codes(original_xi_y_words, xi_codes)
         load_scales(original_xi_y_scales, xi_scales)
-        for t in range(PACK):
-            load_quarter(3, t)
+        load_quarters(3, 0, 2)
+        load_quarters(3, 2, 4)
         nc.sync.dma_start(out=gain[:], in_=gamma_o)
         nc.sync.dma_start(out=bias[:], in_=beta_o)
         nc.sync.dma_start(out=gain_sum[:], in_=gamma_o_sum.partition_broadcast(BATCH))
@@ -133,23 +135,43 @@ def tile_selfprojection_pa_t_kernel(
         column_sums = [[] for batch in range(BATCH)]
         z_psum = {}
 
+        x_sorted = {}
+
+        def sort_words(block, t):
+            x_sorted[block, t] = sort_pool.tile([P, K_PASSES * PAIRS * P], F32, name="x_sorted")
+            nc.vector.tensor_copy(
+                out=x_sorted[block, t][:].rearrange("p (g u w) -> p g u w", g=K_PASSES, u=PAIRS),
+                in_=x_rows[block][:, t, :].bitcast(F32).rearrange("p (g w u) -> p g u w", g=K_PASSES, u=PAIRS),
+            )
+
         def transpose_block(block, chores):
             x_codes[block] = ring.tile([P, PACK, K_PASSES, P], U32, name="x_codes", align_bytes=64)
             x_scales[block] = ring.tile([P, PACK, K_PASSES, P], U8, name="x_scales", align_bytes=64)
             for t in range(PACK):
-                words = x_rows[block][:, t, :].bitcast(F32)
+                in_order = (block, t) in x_sorted
+                words = x_sorted[block, t][:] if in_order else x_rows[block][:, t, :].bitcast(F32)
                 flipped = flip_psum.tile([P, K_PASSES, PAIRS, P], F32, name="flipped")
                 for g in range(K_PASSES):
                     for u in range(PAIRS):
-                        part = words[:, WORDS_PASS * g + u : WORDS_PASS * (g + 1) : PAIRS]
+                        part = (
+                            words[:, WORDS_PASS * g + P * u : WORDS_PASS * g + P * (u + 1)]
+                            if in_order
+                            else words[:, WORDS_PASS * g + u : WORDS_PASS * (g + 1) : PAIRS]
+                        )
                         nc.tensor.transpose(flipped[:, g, u, :], part, identity[:])
-                grouped = stage.tile([P, K_PASSES, P, PACK], BF16, name="grouped", align_bytes=64)
-                nc.scalar.copy(out=grouped[:].bitcast(F32), in_=flipped[:].rearrange("p g u r -> p g r u"))
-                nc.vector.quantize_mx(
-                    out=x_codes[block][:, t].rearrange("p g r -> p (g r)").bitcast(FP8X4),
-                    scales=x_scales[block][:, t].rearrange("p g r -> p (g r)"),
-                    in_=grouped[:].rearrange("p g r v -> p (g r v)"),
+                wide = 2 if 2 <= block < BLOCKS - 1 else 1
+                if t % wide == 0:
+                    grouped = stage.tile([P, 2, K_PASSES, P, PACK], BF16, name="grouped", align_bytes=64)
+                nc.scalar.copy(
+                    out=grouped[:, t % wide].bitcast(F32), in_=flipped[:].rearrange("p g u r -> p g r u")
                 )
+                if t % wide == wide - 1:
+                    done = slice(t + 1 - wide, t + 1)
+                    nc.vector.quantize_mx(
+                        out=x_codes[block][:, done].rearrange("p t g r -> p (t g r)").bitcast(FP8X4),
+                        scales=x_scales[block][:, done].rearrange("p t g r -> p (t g r)"),
+                        in_=grouped[:, 0:wide].rearrange("p t g r v -> p (t g r v)"),
+                    )
                 for chore in chores[t]:
                     chore()
 
@@ -168,8 +190,21 @@ def tile_selfprojection_pa_t_kernel(
                         stop=(g == K_PASSES - 1),
                     )
 
+        def sum_rows(out, block, first, stop):
+            passes = [(t, g) for t in range(PACK) for g in range(K_PASSES)]
+            for i, (t, g) in enumerate(passes):
+                nc.tensor.matmul_mx(
+                    out=out,
+                    lhsT=x_codes[block][:, t, g, :].bitcast(FP8X4),
+                    lhsT_scale=x_scales[block][:, t, g, :],
+                    rhs=xj_codes[:, g, :].bitcast(FP8X4),
+                    rhs_scale=xj_scales[:, g, :],
+                    start=(first and i == 0),
+                    stop=(stop and i == len(passes) - 1),
+                )
+
         def scalar_rounds(block):
-            return block % 4 != 0 or block >= BLOCKS - 3
+            return block % 2 == 1 or block >= BLOCKS - 3
 
         def round_y(block):
             y_grouped[block] = stage.tile([P, P, PACK], BF16, name="y_rounded", align_bytes=64)
@@ -240,23 +275,25 @@ def tile_selfprojection_pa_t_kernel(
             nc.vector.bn_aggr(out=z_stats[batch][:], in_=z_six[batch][:])
 
         def spread_rows(batch):
-            if batch < BATCH - 1:
-                spread_psum[batch] = sums_pool.tile([P, 3, P], F32, name="sums_psum")
+            if batch < BATCH - 2:
+                sums = sums_pool.tile([P, 3, P], F32, name="sums_psum")
+                spread_psum[batch] = [sums[:, i, :] for i in range(3)]
             else:
-                flipped = flip_psum.tile([P, K_PASSES, PAIRS, P], F32, name="flipped")
-                spread_psum[batch] = flipped[:].rearrange("p g u r -> p (g u) r")
+                means = flip_psum.tile([P, K_PASSES, PAIRS, P], F32, name="flipped")
+                others = flip_psum.tile([P, K_PASSES, PAIRS, P], F32, name="flipped")
+                spread_psum[batch] = [means[:, 0, 0, :], others[:, 0, 0, :], others[:, 0, 1, :]]
             for i in range(2):
                 nc.tensor.transpose(
-                    spread_psum[batch][:, i, :], z_stats[batch][:, i : i + 1].to_broadcast([P, P]), identity[:]
+                    spread_psum[batch][i], z_stats[batch][:, i : i + 1].to_broadcast([P, P]), identity[:]
                 )
             if batch < BATCH - 1:
-                nc.tensor.transpose(spread_psum[batch][:, 2, :], column_sums[batch][0][:], identity[:])
+                nc.tensor.transpose(spread_psum[batch][2], column_sums[batch][0][:], identity[:])
 
         def sum_c(batch):
             scratch = ring.tile([P, P], F32, name="scratch")
             nc.scalar.activation(
                 out=scratch[:],
-                in_=spread_psum[batch][:, 2, :],
+                in_=spread_psum[batch][2],
                 func=ACT.Copy,
                 accum_out=c_columns[:, batch : batch + 1],
             )
@@ -265,12 +302,12 @@ def tile_selfprojection_pa_t_kernel(
             scratch = ring.tile([P, P], F32, name="scratch")
             variance_sum[batch] = ring.tile([P, 1], F32, name="variance_sum")
             nc.scalar.activation(
-                out=scratch[:], in_=spread_psum[batch][:, 1, :], func=ACT.Copy, accum_out=variance_sum[batch][:]
+                out=scratch[:], in_=spread_psum[batch][1], func=ACT.Copy, accum_out=variance_sum[batch][:]
             )
 
         def mean_row_stats(batch):
             mean_six[batch] = ring.tile([P, 6], F32, name="mean_six")
-            nc.vector.bn_stats(out=mean_six[batch][:], in_=spread_psum[batch][:, 0, :])
+            nc.vector.bn_stats(out=mean_six[batch][:], in_=spread_psum[batch][0])
 
         def mean_row_aggregate(batch):
             mean_stats[batch] = ring.tile([P, 2], F32, name="mean_stats")
@@ -353,6 +390,9 @@ def tile_selfprojection_pa_t_kernel(
             if step == BLOCKS - 1:
                 round_y(block)
                 sum_y(block)
+            if 5 <= step + 2 < BLOCKS:
+                for t, slot in zip((0,), (3,)):
+                    plan(chores[slot], functools.partial(sort_words, step + 2), t)
             if step == BLOCKS - 4:
                 chores[3].append(prepare)
             transpose_block(step, chores)
@@ -367,12 +407,15 @@ def tile_selfprojection_pa_t_kernel(
 
         third, last = BATCH - 2, BATCH - 1
         final = BLOCKS - 1
+        tail_sums = sums_pool.tile([P, 3, P], F32, name="sums_psum")
+        sum_rows(tail_sums[:, 0, :], final - 1, True, False)
         quantize_y(final - 2)
         project_block(final)
+        sum_rows(tail_sums[:, 0, :], final, False, True)
         contract_block(final - 2)
         row_stats(third)
+        add_y(final - 2)
         round_y(final - 1)
-        sum_y(final - 1)
         row_aggregate(third)
         quantize_y(final - 1)
         spread_rows(third)
@@ -380,55 +423,51 @@ def tile_selfprojection_pa_t_kernel(
         round_y(final)
         quantize_y(final)
         contract_block(final)
-        sum_variances(third)
+        total = column_sums[last][0]
+        nc.vector.tensor_tensor(out=total[:], in0=tail_sums[:, 0, :], in1=total[:], op=ALU.add)
+        c_psum = flip_psum.tile([P, K_PASSES, PAIRS, P], F32, name="flipped")
+        nc.tensor.matmul(out=c_psum[:, 0, 0, :], lhsT=selector[:], rhs=total[:], start=True, stop=True)
         sum_c(third)
-        sum_y(final)
+        mean_row_stats(third)
         z_source[last] = z_psum[last]
         row_stats(last)
-        add_y(final - 2)
-        row_aggregate(last)
-        add_y(final - 1)
         c_early_psum = flip_psum.tile([P, K_PASSES, PAIRS, P], F32, name="flipped")
         nc.tensor.transpose(c_early_psum[:, 0, 0, :], c_columns[:], identity[:])
-        spread_rows(last)
+        sum_variances(third)
+        mean_row_aggregate(third)
+        row_aggregate(last)
         c_early = keep.tile([BATCH, P], F32)
         nc.scalar.copy(out=c_early[:], in_=c_early_psum[0:BATCH, 0, 0, :])
-        mean_row_stats(third)
-        add_y(final)
-        sum_variances(last)
-        c_psum = flip_psum.tile([P, K_PASSES, PAIRS, P], F32, name="flipped")
-        nc.tensor.matmul(
-            out=c_psum[:, 0, 0, :], lhsT=selector[:], rhs=column_sums[last][0][:], start=True, stop=True
-        )
-        mean_row_aggregate(third)
-        mean_row_stats(last)
+        spread_rows(last)
         total_variance(third)
         take_root(third)
-        mean_row_aggregate(last)
-        gain_z(third)
-        total_variance(last)
-        take_root(last)
-        gain_z(last)
-        add_eps(third)
-        add_eps(last)
         c = keep.tile([BATCH, P], F32)
         nc.vector.tensor_tensor(out=c[:], in0=c_psum[0:BATCH, 0, 0, :], in1=c_early[:], op=ALU.add)
-        invert(third)
-        invert(last)
+        gain_z(third)
+        mean_row_stats(last)
+        sum_variances(last)
         c_six = ring.tile([BATCH, 6], F32, name="c_six")
         nc.vector.bn_stats(out=c_six[:], in_=c[:])
-        finish_z(last)
+        mean_row_aggregate(last)
+        add_eps(third)
+        total_variance(last)
+        take_root(last)
         c_stats = ring.tile([BATCH, 2], F32, name="c_stats")
         nc.vector.bn_aggr(out=c_stats[:], in_=c_six[:])
+        gain_z(last)
         c_spread = ring.tile([BATCH, 1], F32, name="c_spread")
         nc.scalar.activation(out=c_spread[:], in_=c_stats[:, 1:2], func=ACT.Sqrt, scale=P / (P - 1.0))
-        finish_z(third)
+        add_eps(last)
         c_gained = ring.tile([BATCH, P], F32, name="c_gained")
         nc.vector.scalar_tensor_tensor(
             out=c_gained[:], in0=c[:], scalar=c_stats[:, 0:1], in1=gain_sum[:], op0=ALU.subtract, op1=ALU.mult
         )
+        invert(last)
         nc.vector.tensor_scalar_add(out=c_spread[:], in0=c_spread[:], scalar1=EPS)
+        invert(third)
+        finish_z(last)
         nc.vector.reciprocal(out=c_spread[:], in_=c_spread[:])
+        finish_z(third)
         o_sum = ring.tile([BATCH, P], F32, name="o_sum")
         nc.vector.scalar_tensor_tensor(
             out=o_sum[:], in0=c_gained[:], scalar=c_spread[:], in1=bias_sum_one[:], op0=ALU.mult, op1=ALU.add

@@ -52,7 +52,6 @@ def tile_selfprojection_pa_t_kernel(
         x_pool = ctx.enter_context(tc.tile_pool(name="x_pool", bufs=BLOCKS))
         stage = ctx.enter_context(tc.tile_pool(name="stage", bufs=4))
         ring = ctx.enter_context(tc.tile_pool(name="ring", bufs=3))
-        sort_pool = ctx.enter_context(tc.tile_pool(name="sort_pool", bufs=6))
         flip_psum = ctx.enter_context(tc.psum_pool(name="flip_psum", bufs=4))
         y_pool = ctx.enter_context(tc.psum_pool(name="y_pool", bufs=2))
         z_pool = ctx.enter_context(tc.psum_pool(name="z_pool", bufs=1))
@@ -135,29 +134,15 @@ def tile_selfprojection_pa_t_kernel(
         column_sums = [[] for batch in range(BATCH)]
         z_psum = {}
 
-        x_sorted = {}
-
-        def sort_words(block, t):
-            x_sorted[block, t] = sort_pool.tile([P, K_PASSES * PAIRS * P], F32, name="x_sorted")
-            nc.vector.tensor_copy(
-                out=x_sorted[block, t][:].rearrange("p (g u w) -> p g u w", g=K_PASSES, u=PAIRS),
-                in_=x_rows[block][:, t, :].bitcast(F32).rearrange("p (g w u) -> p g u w", g=K_PASSES, u=PAIRS),
-            )
-
         def transpose_block(block, chores):
             x_codes[block] = ring.tile([P, PACK, K_PASSES, P], U32, name="x_codes", align_bytes=64)
             x_scales[block] = ring.tile([P, PACK, K_PASSES, P], U8, name="x_scales", align_bytes=64)
             for t in range(PACK):
-                in_order = (block, t) in x_sorted
-                words = x_sorted[block, t][:] if in_order else x_rows[block][:, t, :].bitcast(F32)
+                words = x_rows[block][:, t, :].bitcast(F32)
                 flipped = flip_psum.tile([P, K_PASSES, PAIRS, P], F32, name="flipped")
                 for g in range(K_PASSES):
                     for u in range(PAIRS):
-                        part = (
-                            words[:, WORDS_PASS * g + P * u : WORDS_PASS * g + P * (u + 1)]
-                            if in_order
-                            else words[:, WORDS_PASS * g + u : WORDS_PASS * (g + 1) : PAIRS]
-                        )
+                        part = words[:, WORDS_PASS * g + u : WORDS_PASS * (g + 1) : PAIRS]
                         nc.tensor.transpose(flipped[:, g, u, :], part, identity[:])
                 wide = 2 if 2 <= block < BLOCKS - 1 else 1
                 if t % wide == 0:
@@ -204,7 +189,7 @@ def tile_selfprojection_pa_t_kernel(
                 )
 
         def scalar_rounds(block):
-            return block % 2 == 1 or block >= BLOCKS - 3
+            return block % 4 == 1 or block >= BLOCKS - 3
 
         def round_y(block):
             y_grouped[block] = stage.tile([P, P, PACK], BF16, name="y_rounded", align_bytes=64)
@@ -390,9 +375,6 @@ def tile_selfprojection_pa_t_kernel(
             if step == BLOCKS - 1:
                 round_y(block)
                 sum_y(block)
-            if 5 <= step + 2 < BLOCKS:
-                for t, slot in zip((0,), (3,)):
-                    plan(chores[slot], functools.partial(sort_words, step + 2), t)
             if step == BLOCKS - 4:
                 chores[3].append(prepare)
             transpose_block(step, chores)

import functools
from contextlib import ExitStack

import concourse.mybir as mybir
from concourse.masks import make_identity

F32 = mybir.dt.float32
BF16 = mybir.dt.bfloat16
I32 = mybir.dt.int32
U32 = mybir.dt.uint32
U8 = mybir.dt.uint8
FP8X4 = mybir.dt.float8_e4m3fn_x4
ALU = mybir.AluOpType
ACT = mybir.ActivationFunctionType
AXIS = mybir.AxisListType

P = 128
PACK = 4
K_PASS = P * PACK
BATCH = 4
ROWS = 2048
K = 1024
K_PASSES = K // K_PASS
ROW_PASSES = ROWS // K_PASS
BLOCKS = BATCH * ROW_PASSES
PAIRS = 2
WORDS_PASS = K_PASS // 2
QUADRANTS = 4
EPS = 1e-05

FLOPS = 2 * BATCH * ROWS * K * P + 2 * BATCH * ROWS * P * P


def tile_selfprojection_pa_t_kernel(
    tc,
    x,
    original_xj_y_words,
    original_xj_y_scales,
    original_xi_y_words,
    original_xi_y_scales,
    gamma_o_sum,
    gamma_o,
    beta_o_sum,
    beta_o,
    out_0,
    out_1,
):
    nc = tc.nc
    with ExitStack() as ctx:
        ctx.enter_context(tc.manual_schedule())
        keep = ctx.enter_context(tc.tile_pool(name="keep", bufs=1))
        x_pool = ctx.enter_context(tc.tile_pool(name="x_pool", bufs=BLOCKS))
        stage = ctx.enter_context(tc.tile_pool(name="stage", bufs=4))
        ring = ctx.enter_context(tc.tile_pool(name="ring", bufs=3))
        flip_psum = ctx.enter_context(tc.psum_pool(name="flip_psum", bufs=4))
        y_pool = ctx.enter_context(tc.psum_pool(name="y_pool", bufs=2))
        z_pool = ctx.enter_context(tc.psum_pool(name="z_pool", bufs=1))
        sums_pool = ctx.enter_context(tc.psum_pool(name="sums_pool", bufs=1))

        xj_scales = keep.tile([P, K_PASSES, P], U8, align_bytes=64)
        xi_scales = keep.tile([P, ROW_PASSES, P], U8, align_bytes=64)
        nc.vector.memset(xj_scales[:].bitcast(I32), 0)
        nc.vector.memset(xi_scales[:].bitcast(I32), 0)
        selector = keep.tile([P, P], F32)
        nc.vector.memset(selector[:], 0.0)
        nc.vector.memset(selector[:, BATCH - 1 : BATCH], 1.0)
        warm = keep.tile([P, 1], F32)
        nc.vector.memset(warm[:], 1.0)
        nc.scalar.activation(out=warm[:], in_=warm[:], func=ACT.Sqrt)
        identity = keep.tile([P, P], F32)
        make_identity(nc, identity[:])
        c_columns = keep.tile([P, P], F32)
        nc.vector.memset(c_columns[:], 0.0)

        x_blocks_hbm = x.rearrange("b (g p t) k -> (b g) p t k", p=P, t=PACK)
        x_rows = []
        for block in range(BLOCKS):
            x_rows.append(x_pool.tile([P, PACK, K], BF16, name="x_rows"))

        def load_quarters(block, first, end):
            nc.sync.dma_start(out=x_rows[block][:, first:end, :], in_=x_blocks_hbm[block, :, first:end, :])

        def load_block(block):
            nc.sync.dma_start(out=x_rows[block][:], in_=x_blocks_hbm[block])

        def load_codes(words_hbm, codes):
            nc.sync.dma_start(
                out=codes[:].bitcast(I32),
                in_=words_hbm.rearrange("g p n t -> p g (n t)").bitcast(I32),
            )

        def load_scales(scales_hbm, scales):
            rows = scales_hbm.rearrange("g q n -> q g n")
            for quadrant in range(QUADRANTS):
                nc.sync.dma_start(
                    out=scales[32 * quadrant : 32 * quadrant + 4].bitcast(I32),
                    in_=rows[4 * quadrant : 4 * quadrant + 4].bitcast(I32),
                )

        xj_codes = keep.tile([P, K_PASSES, P], U32, align_bytes=64)
        xi_codes = keep.tile([P, ROW_PASSES, P], U32, align_bytes=64)
        gain = keep.tile([P, P], BF16)
        bias = keep.tile([P, P], BF16)
        gain_sum = keep.tile([BATCH, P], BF16)
        bias_sum = keep.tile([BATCH, P], BF16)
        bias_sum_one = keep.tile([BATCH, P], F32)

        load_quarters(0, 0, 1)
        load_quarters(0, 1, 2)
        load_quarters(0, 2, 4)
        load_codes(original_xj_y_words, xj_codes)
        load_scales(original_xj_y_scales, xj_scales)
        for block in (1, 2):
            load_quarters(block, 0, 2)
            load_quarters(block, 2, 4)
        load_codes(original_xi_y_words, xi_codes)
        load_scales(original_xi_y_scales, xi_scales)
        load_quarters(3, 0, 2)
        load_quarters(3, 2, 4)
        nc.sync.dma_start(out=gain[:], in_=gamma_o)
        nc.sync.dma_start(out=bias[:], in_=beta_o)
        nc.sync.dma_start(out=gain_sum[:], in_=gamma_o_sum.partition_broadcast(BATCH))
        nc.sync.dma_start(out=bias_sum[:], in_=beta_o_sum.partition_broadcast(BATCH))
        for block in range(4, BLOCKS):
            load_block(block)

        x_codes = {}
        x_scales = {}
        y_by_column = {}
        block_sums = {}
        y_grouped = {}
        y_codes = {}
        y_scales = {}
        column_sums = [[] for batch in range(BATCH)]
        z_psum = {}

        def transpose_block(block, chores):
            x_codes[block] = ring.tile([P, PACK, K_PASSES, P], U32, name="x_codes", align_bytes=64)
            x_scales[block] = ring.tile([P, PACK, K_PASSES, P], U8, name="x_scales", align_bytes=64)
            for t in range(PACK):
                words = x_rows[block][:, t, :].bitcast(F32)
                flipped = flip_psum.tile([P, K_PASSES, PAIRS, P], F32, name="flipped")
                for g in range(K_PASSES):
                    for u in range(PAIRS):
                        part = words[:, WORDS_PASS * g + u : WORDS_PASS * (g + 1) : PAIRS]
                        nc.tensor.transpose(flipped[:, g, u, :], part, identity[:])
                wide = 2 if 2 <= block < BLOCKS - 1 else 1
                if t % wide == 0:
                    grouped = stage.tile([P, 2, K_PASSES, P, PACK], BF16, name="grouped", align_bytes=64)
                nc.scalar.copy(
                    out=grouped[:, t % wide].bitcast(F32), in_=flipped[:].rearrange("p g u r -> p g r u")
                )
                if t % wide == wide - 1:
                    done = slice(t + 1 - wide, t + 1)
                    nc.vector.quantize_mx(
                        out=x_codes[block][:, done].rearrange("p t g r -> p (t g r)").bitcast(FP8X4),
                        scales=x_scales[block][:, done].rearrange("p t g r -> p (t g r)"),
                        in_=grouped[:, 0:wide].rearrange("p t g r v -> p (t g r v)"),
                    )
                for chore in chores[t]:
                    chore()

        def project_block(block):
            y_psum = y_pool.tile([P, PACK, P], F32, name="y_psum")
            y_by_column[block] = y_psum[:].rearrange("p t j -> p j t")
            for t in range(PACK):
                for g in range(K_PASSES):
                    nc.tensor.matmul_mx(
                        out=y_psum[:, t, :],
                        lhsT=x_codes[block][:, t, g, :].bitcast(FP8X4),
                        lhsT_scale=x_scales[block][:, t, g, :],
                        rhs=xj_codes[:, g, :].bitcast(FP8X4),
                        rhs_scale=xj_scales[:, g, :],
                        start=(g == 0),
                        stop=(g == K_PASSES - 1),
                    )

        def sum_rows(out, block, first, stop):
            passes = [(t, g) for t in range(PACK) for g in range(K_PASSES)]
            for i, (t, g) in enumerate(passes):
                nc.tensor.matmul_mx(
                    out=out,
                    lhsT=x_codes[block][:, t, g, :].bitcast(FP8X4),
                    lhsT_scale=x_scales[block][:, t, g, :],
                    rhs=xj_codes[:, g, :].bitcast(FP8X4),
                    rhs_scale=xj_scales[:, g, :],
                    start=(first and i == 0),
                    stop=(stop and i == len(passes) - 1),
                )

        def scalar_rounds(block):
            return block % 4 == 1 or block >= BLOCKS - 3

        def round_y(block):
            y_grouped[block] = stage.tile([P, P, PACK], BF16, name="y_rounded", align_bytes=64)
            if scalar_rounds(block):
                nc.scalar.copy(out=y_grouped[block][:], in_=y_by_column[block])
            else:
                nc.vector.tensor_copy(out=y_grouped[block][:], in_=y_by_column[block])

        def sum_y(block):
            batch, row_pass = divmod(block, ROW_PASSES)
            by_column = y_by_column[block]
            sums = keep.tile([P, P], F32, name="block_sums_%d" % block)
            nc.vector.tensor_reduce(out=sums[:], in_=by_column, axis=AXIS.X, op=ALU.add)
            block_sums[block] = sums

        def add_y(block):
            batch, row_pass = divmod(block, ROW_PASSES)
            sums = block_sums[block]
            if row_pass == 0:
                column_sums[batch].append(sums)
            else:
                total = column_sums[batch][0]
                nc.vector.tensor_tensor(out=total[:], in0=total[:], in1=sums[:], op=ALU.add)

        def quantize_y(block):
            y_codes[block] = ring.tile([P, P], U32, name="y_codes", align_bytes=64)
            y_scales[block] = ring.tile([P, P], U8, name="y_scales", align_bytes=64)
            nc.vector.quantize_mx(
                out=y_codes[block][:].bitcast(FP8X4),
                scales=y_scales[block][:],
                in_=y_grouped[block][:].rearrange("p j t -> p (j t)"),
            )

        def contract_block(block):
            batch, row_pass = divmod(block, ROW_PASSES)
            if row_pass == 0:
                z_psum[batch] = z_pool.tile([P, P], F32, name="z_psum")
            nc.tensor.matmul_mx(
                out=z_psum[batch][:],
                lhsT=xi_codes[:, row_pass, :].bitcast(FP8X4),
                lhsT_scale=xi_scales[:, row_pass, :],
                rhs=y_codes[block][:].bitcast(FP8X4),
                rhs_scale=y_scales[block][:],
                start=(row_pass == 0),
                stop=(row_pass == ROW_PASSES - 1),
            )

        z_source = {}
        z_six = {}
        z_stats = {}
        spread_psum = {}
        mean_six = {}
        mean_stats = {}
        variance_sum = {}
        z_spread = {}
        z_gained = {}

        def save_z(batch):
            z_source[batch] = ring.tile([P, P], F32, name="z_sbuf")
            nc.scalar.copy(out=z_source[batch][:], in_=z_psum[batch][:])

        def row_stats(batch):
            z_six[batch] = ring.tile([P, 6], F32, name="z_six")
            nc.vector.bn_stats(out=z_six[batch][:], in_=z_source[batch][:])

        def row_aggregate(batch):
            z_stats[batch] = ring.tile([P, 2], F32, name="z_stats")
            nc.vector.bn_aggr(out=z_stats[batch][:], in_=z_six[batch][:])

        def spread_rows(batch):
            if batch < BATCH - 2:
                sums = sums_pool.tile([P, 3, P], F32, name="sums_psum")
                spread_psum[batch] = [sums[:, i, :] for i in range(3)]
            else:
                means = flip_psum.tile([P, K_PASSES, PAIRS, P], F32, name="flipped")
                others = flip_psum.tile([P, K_PASSES, PAIRS, P], F32, name="flipped")
                spread_psum[batch] = [means[:, 0, 0, :], others[:, 0, 0, :], others[:, 0, 1, :]]
            for i in range(2):
                nc.tensor.transpose(
                    spread_psum[batch][i], z_stats[batch][:, i : i + 1].to_broadcast([P, P]), identity[:]
                )
            if batch < BATCH - 1:
                nc.tensor.transpose(spread_psum[batch][2], column_sums[batch][0][:], identity[:])

        def sum_c(batch):
            scratch = ring.tile([P, P], F32, name="scratch")
            nc.scalar.activation(
                out=scratch[:],
                in_=spread_psum[batch][2],
                func=ACT.Copy,
                accum_out=c_columns[:, batch : batch + 1],
            )

        def sum_variances(batch):
            scratch = ring.tile([P, P], F32, name="scratch")
            variance_sum[batch] = ring.tile([P, 1], F32, name="variance_sum")
            nc.scalar.activation(
                out=scratch[:], in_=spread_psum[batch][1], func=ACT.Copy, accum_out=variance_sum[batch][:]
            )

        def mean_row_stats(batch):
            mean_six[batch] = ring.tile([P, 6], F32, name="mean_six")
            nc.vector.bn_stats(out=mean_six[batch][:], in_=spread_psum[batch][0])

        def mean_row_aggregate(batch):
            mean_stats[batch] = ring.tile([P, 2], F32, name="mean_stats")
            nc.vector.bn_aggr(out=mean_stats[batch][:], in_=mean_six[batch][:])

        def total_variance(batch):
            z_spread[batch] = ring.tile([P, 1], F32, name="z_spread")
            nc.vector.scalar_tensor_tensor(
                out=z_spread[batch][:],
                in0=variance_sum[batch][:],
                scalar=1.0 / P,
                in1=mean_stats[batch][:, 1:2],
                op0=ALU.mult,
                op1=ALU.add,
            )

        def take_root(batch):
            nc.scalar.activation(
                out=z_spread[batch][:], in_=z_spread[batch][:], func=ACT.Sqrt, scale=P * P / (P * P - 1.0)
            )

        def gain_z(batch):
            z_gained[batch] = ring.tile([P, P], F32, name="z_gained")
            nc.vector.scalar_tensor_tensor(
                out=z_gained[batch][:],
                in0=z_source[batch][:],
                scalar=mean_stats[batch][:, 0:1],
                in1=gain[:],
                op0=ALU.subtract,
                op1=ALU.mult,
            )

        def add_eps(batch):
            nc.vector.tensor_scalar_add(out=z_spread[batch][:], in0=z_spread[batch][:], scalar1=EPS)

        def invert(batch):
            nc.vector.reciprocal(out=z_spread[batch][:], in_=z_spread[batch][:])

        def finish_z(batch):
            result = ring.tile([P, P], F32, name="result")
            nc.vector.scalar_tensor_tensor(
                out=result[:], in0=z_gained[batch][:], scalar=z_spread[batch][:], in1=bias[:], op0=ALU.mult, op1=ALU.add
            )
            nc.sync.dma_start(out=out_0[batch], in_=result[:])

        def prepare():
            nc.vector.tensor_scalar_add(out=bias_sum_one[:], in0=bias_sum[:], scalar1=1.0)

        def plan(where, work, item):
            where.append(functools.partial(work, item))

        for step in range(BLOCKS):
            chores = ([], [], [], [])
            late = []
            for batch in range(BATCH - 2):
                done = ROW_PASSES * (batch + 1) + 2
                if step == done + 1:
                    plan(chores[0], row_stats, batch)
                    plan(chores[1], row_aggregate, batch)
                if step == done + 2:
                    plan(late, spread_rows, batch)
                if step == done + 3:
                    plan(chores[0], sum_variances, batch)
                    plan(chores[0], mean_row_stats, batch)
                    plan(chores[1], sum_c, batch)
                    plan(chores[1], mean_row_aggregate, batch)
                    plan(chores[2], total_variance, batch)
                    plan(chores[3], take_root, batch)
                if step == done + 4:
                    plan(chores[0], gain_z, batch)
                    plan(chores[1], add_eps, batch)
                    plan(chores[2], invert, batch)
                    plan(chores[3], finish_z, batch)
            block = step - 2
            if 0 <= block < BLOCKS - 3:
                plan(chores[0], round_y, block)
                plan(chores[1], sum_y, block)
                plan(chores[2], quantize_y, block)
                plan(chores[2], add_y, block)
            if step == BLOCKS - 1:
                round_y(block)
                sum_y(block)
            if step == BLOCKS - 4:
                chores[3].append(prepare)
            transpose_block(step, chores)
            for task in late:
                task()
            if step >= 3:
                contract_block(step - 3)
                if step % ROW_PASSES == 2:
                    save_z((step - 3) // ROW_PASSES)
            if step >= 1:
                project_block(step - 1)

        third, last = BATCH - 2, BATCH - 1
        final = BLOCKS - 1
        tail_sums = sums_pool.tile([P, 3, P], F32, name="sums_psum")
        sum_rows(tail_sums[:, 0, :], final - 1, True, False)
        quantize_y(final - 2)
        project_block(final)
        sum_rows(tail_sums[:, 0, :], final, False, True)
        contract_block(final - 2)
        row_stats(third)
        add_y(final - 2)
        round_y(final - 1)
        row_aggregate(third)
        quantize_y(final - 1)
        spread_rows(third)
        contract_block(final - 1)
        round_y(final)
        quantize_y(final)
        contract_block(final)
        total = column_sums[last][0]
        nc.vector.tensor_tensor(out=total[:], in0=tail_sums[:, 0, :], in1=total[:], op=ALU.add)
        c_psum = flip_psum.tile([P, K_PASSES, PAIRS, P], F32, name="flipped")
        nc.tensor.matmul(out=c_psum[:, 0, 0, :], lhsT=selector[:], rhs=total[:], start=True, stop=True)
        sum_c(third)
        mean_row_stats(third)
        z_source[last] = z_psum[last]
        row_stats(last)
        c_early_psum = flip_psum.tile([P, K_PASSES, PAIRS, P], F32, name="flipped")
        nc.tensor.transpose(c_early_psum[:, 0, 0, :], c_columns[:], identity[:])
        sum_variances(third)
        mean_row_aggregate(third)
        row_aggregate(last)
        c_early = keep.tile([BATCH, P], F32)
        nc.scalar.copy(out=c_early[:], in_=c_early_psum[0:BATCH, 0, 0, :])
        spread_rows(last)
        total_variance(third)
        take_root(third)
        c = keep.tile([BATCH, P], F32)
        nc.vector.tensor_tensor(out=c[:], in0=c_psum[0:BATCH, 0, 0, :], in1=c_early[:], op=ALU.add)
        gain_z(third)
        mean_row_stats(last)
        sum_variances(last)
        c_six = ring.tile([BATCH, 6], F32, name="c_six")
        nc.vector.bn_stats(out=c_six[:], in_=c[:])
        mean_row_aggregate(last)
        add_eps(third)
        total_variance(last)
        take_root(last)
        c_stats = ring.tile([BATCH, 2], F32, name="c_stats")
        nc.vector.bn_aggr(out=c_stats[:], in_=c_six[:])
        gain_z(last)
        c_spread = ring.tile([BATCH, 1], F32, name="c_spread")
        nc.scalar.activation(out=c_spread[:], in_=c_stats[:, 1:2], func=ACT.Sqrt, scale=P / (P - 1.0))
        add_eps(last)
        c_gained = ring.tile([BATCH, P], F32, name="c_gained")
        nc.vector.scalar_tensor_tensor(
            out=c_gained[:], in0=c[:], scalar=c_stats[:, 0:1], in1=gain_sum[:], op0=ALU.subtract, op1=ALU.mult
        )
        invert(last)
        nc.vector.tensor_scalar_add(out=c_spread[:], in0=c_spread[:], scalar1=EPS)
        invert(third)
        finish_z(last)
        nc.vector.reciprocal(out=c_spread[:], in_=c_spread[:])
        finish_z(third)
        o_sum = ring.tile([BATCH, P], F32, name="o_sum")
        nc.vector.scalar_tensor_tensor(
            out=o_sum[:], in0=c_gained[:], scalar=c_spread[:], in1=bias_sum_one[:], op0=ALU.mult, op1=ALU.add
        )
        nc.sync.dma_start(out=out_1, in_=o_sum[:])
